import numpy as np
import ml_dtypes


def mxq(x, axis, fmt="e4m3"):
    dtype, down = {"e4m3": (ml_dtypes.float8_e4m3fn, 7), "e5m2": (ml_dtypes.float8_e5m2, 14)}[fmt]
    v = np.moveaxis(np.asarray(x, np.float32).astype(ml_dtypes.bfloat16).astype(np.float64), axis, -1)
    blocks = v.reshape(v.shape[:-1] + (-1, 32))
    amax = np.abs(blocks).max(-1, keepdims=True)
    byte = np.maximum(np.where(amax > 0, np.frexp(amax)[1] - 1 + 127, 0) - down, 1)
    scale = np.exp2(byte - 127.0)
    codes = (blocks / scale).astype(np.float32).astype(dtype).astype(np.float64)
    return np.moveaxis((codes * scale).reshape(v.shape), -1, axis)


WIDE = False


def mx_kscale(k):
    if not WIDE:
        return np.ones(k)
    levels = np.array([10, -10, 5, -5, 0])
    if k % 512:
        return np.exp2(np.random.permutation(np.resize(levels, k // 32))).repeat(32)
    a = np.empty((k // 512, 16))
    for p in range(k // 512):
        a[p, :8] = np.random.permutation(np.resize(levels, 8))
        for g in range(8):
            far = levels[np.abs(levels - a[p, g]) >= 10]
            a[p, g + 8] = far[np.random.randint(len(far))]
    return np.exp2(a.ravel()).repeat(32)


BF16 = ml_dtypes.bfloat16


def bf(x):
    return np.asarray(x, np.float32).astype(BF16)


def f64(x):
    return np.asarray(x).astype(np.float64)


T, B, E, CDIM, H, K = 512, 4, 1024, 1024, 16, 32
R = CDIM // H
EPS = 1e-5


def layer_norm(v, g, b):
    m = v.mean(-1, keepdims=True)
    var = ((v - m) ** 2).mean(-1, keepdims=True)
    return (v - m) * (1.0 / np.sqrt(var + EPS)) * g + b


def setup_inputs():
    s = mx_kscale(CDIM)
    return {"h": bf(np.random.standard_normal((T, B, CDIM)) * s),
            "x": bf(np.random.standard_normal((T, B, E))),
            "ww": bf(np.random.standard_normal((H * K, CDIM)) / np.sqrt(CDIM) / s),
            "bw": bf(np.random.standard_normal(H * K) * 0.5),
            "w2": bf(np.random.standard_normal((E, CDIM)) * 3.0 / np.sqrt(CDIM) / s),
            "b2": bf(np.random.standard_normal(E) * 0.2),
            "gamma": bf(1.0 + 0.1 * np.random.standard_normal(E)),
            "beta": bf(np.random.standard_normal(E) * 0.2)}


def reference(h, x, ww, bw, w2, b2, gamma, beta):
    h = f64(h)
    z = ((mxq(h, 2, "e4m3") @ mxq(f64(ww).T, 0, "e4m3")) + f64(bw)).reshape(T, B, H, K)
    e = np.exp(z - z.max(-1, keepdims=True))
    w = e / e.sum(-1, keepdims=True)
    hp = np.concatenate([np.zeros((K - 1, B, H, R)), h.reshape(T, B, H, R)], 0)
    acc = np.zeros((T, B, H, R))
    for k in range(K):
        acc = acc + w[:, :, :, k:k + 1] * hp[k:k + T]
    c = acc.reshape(T, B, CDIM)
    y = (mxq(c, 2, "e4m3") @ mxq(f64(w2).T, 0, "e4m3")) + f64(b2)
    return layer_norm(f64(x) + y, f64(gamma), f64(beta))

@@ -1,0 +1,468 @@
+from contextlib import ExitStack
+
+import concourse.mybir as mybir
+from concourse.masks import make_identity
+
+FLOPS = 6576668672
+F32 = mybir.dt.float32
+BF16 = mybir.dt.bfloat16
+U32 = mybir.dt.uint32
+U8 = mybir.dt.uint8
+FP8X4 = mybir.dt.float8_e4m3fn_x4
+ALU = mybir.AluOpType
+ACT = mybir.ActivationFunctionType
+AX = mybir.AxisListType
+
+P = 128
+NB = 4
+NI = 4
+NT = NB * NI
+C = 1024
+H = 16
+K = 32
+R = 64
+CH = 63
+EPS = 1e-5
+NBAND = 3
+PINNED = True
+
+
+def tile_dynamicconvdecoderlayer_pa_kernel(tc, h, x, ww, bw, w2, b2, gamma, beta, out):
+    nc = tc.nc
+    with ExitStack() as ctx:
+        const = ctx.enter_context(tc.tile_pool(name="const", bufs=1))
+        wst = ctx.enter_context(tc.tile_pool(name="wst", bufs=4))
+        p2 = ctx.enter_context(tc.tile_pool(name="p2", bufs=2))
+        p3 = ctx.enter_context(tc.tile_pool(name="p3", bufs=3))
+        hfp = ctx.enter_context(tc.tile_pool(name="hfp", bufs=7))
+        p1 = ctx.enter_context(tc.tile_pool(name="p1", bufs=1))
+        ps_t = ctx.enter_context(tc.psum_pool(name="ps_t", bufs=3))
+        ps_z = ctx.enter_context(tc.psum_pool(name="ps_z", bufs=1))
+        ps_c = ctx.enter_context(tc.psum_pool(name="ps_c", bufs=2))
+        ps_y = ctx.enter_context(tc.psum_pool(name="ps_y", bufs=2))
+        if PINNED:
+            ctx.enter_context(tc.manual_schedule())
+
+        flat = out.rearrange("t b e -> (t b e)")
+        T = {}
+
+        def ok(t):
+            return 0 <= t < NT
+
+        idf = const.tile([P, 2 * P], F32, name="idf")
+        make_identity(nc, idf[:, 0:P])
+        nc.vector.tensor_copy(out=idf[:, P:2 * P], in_=idf[:, 0:P])
+        idb = const.tile([P, 2 * P], BF16, name="idb")
+        nc.vector.tensor_copy(out=idb[:], in_=idf[:])
+        msk = const.tile([P, 4], F32, name="msk")
+        nc.vector.tensor_reduce(out=msk[:], in_=idf[:, 0:P].rearrange("p (j c) -> p j c", c=32), axis=AX.X, op=ALU.add)
+        nhalf = const.tile([P, 1], F32, name="nhalf")
+        nc.vector.memset(nhalf[:], -0.5)
+        bw_bc = const.tile([P, H * K], BF16, name="bw_bc")
+        b2_bc = const.tile([P, C], BF16, name="b2_bc")
+        g_bc = const.tile([P, C], BF16, name="g_bc")
+        be_bc = const.tile([P, C], BF16, name="be_bc")
+        wwq = const.tile([P, 2, 512], U32, name="wwq", align_bytes=64)
+        wws = const.tile([P, 2, 512], U8, name="wws", align_bytes=64)
+        w2q = const.tile([P, 2, 1024], U32, name="w2q", align_bytes=64)
+        w2s = const.tile([P, 2, 1024], U8, name="w2s", align_bytes=64)
+        gww = const.tile([P, 4096], BF16, name="gww", align_bytes=64)
+        gww32 = gww[:].bitcast(F32).rearrange("p (g c u) -> p g c u", g=2, u=2)
+        gw2 = const.tile([P, 8192], BF16, name="gw2", align_bytes=64)
+        gw2v = gw2[:].rearrange("p (g c t) -> p g c t", g=2, t=4)
+        stages = [const.tile([P, 1024], F32, name="stage%d" % i) for i in range(3)]
+        bands = [const.tile([P, H, P], F32, name="band%d" % i) for i in range(NBAND)]
+        corners = [const.tile([P, 4, P], F32, name="corner%d" % i) for i in range(NBAND)]
+
+        def ld(t):
+            if not ok(t):
+                return
+            hb = p3.tile([P, C], BF16, name="hb", tag="hb")
+            nc.sync.dma_start(out=hb[:], in_=h[P * (t // NB):P * (t // NB) + P, t % NB, :])
+            T[("hb", t)] = hb
+
+        def ld_x(t):
+            if not ok(t):
+                return
+            xt = p3.tile([P, C], BF16, name="xt", tag="xt")
+            nc.sync.dma_start(out=xt[:], in_=x[P * (t // NB):P * (t // NB) + P, t % NB, :])
+            T[("xt", t)] = xt
+
+        def ld_hc(ib):
+            hcb = p2.tile([P, NB, 256], BF16, name="hcb", tag="hcb")
+            for j in range(4):
+                nc.sync.dma_start(out=hcb[32 * j:32 * j + 32, :, :], in_=h[P * ib - 32:P * ib, :, 256 * j:256 * j + 256])
+            T[("hcb", ib)] = hcb
+
+        raws = []
+        for rt in range(4):
+            raw = wst.tile([P, C], BF16, name="raw", tag="raw")
+            nc.sync.dma_start(out=raw[:], in_=ww[P * rt:P * rt + P, :])
+            raws.append(raw)
+        ld(0)
+        nc.sync.dma_start(out=bw_bc[:], in_=bw.partition_broadcast(P))
+        for st in stages:
+            nc.vector.memset(st[:], 0.0)
+        for rt in range(4):
+            tp = ps_t.tile([P, 4, P], F32, name="tp", tag="tp")
+            for gu in range(4):
+                g, u = divmod(gu, 2)
+                nc.tensor.transpose(tp[:, gu, :], raws[rt][:].bitcast(F32)[:, 256 * g + u:256 * g + 256:2], idf[:, 0:P])
+            if rt % 2 == 0:
+                nc.vector.tensor_copy(out=gww32[:, :, P * rt:P * rt + P, :], in_=tp[:].rearrange("p (g u) r -> p g r u", g=2))
+            else:
+                nc.scalar.copy(out=gww32[:, :, P * rt:P * rt + P, :], in_=tp[:].rearrange("p (g u) r -> p g r u", g=2))
+        for g in range(2):
+            nc.vector.quantize_mx(out=wwq[:, g, :].bitcast(FP8X4), scales=wws[:, g, :], in_=gww[:, 2048 * g:2048 * g + 2048])
+        nc.vector.memset(bands[0][:], 0.0)
+
+        def pe_hT(t):
+            if not ok(t):
+                return
+            tp = ps_t.tile([P, 4, P], F32, name="tp", tag="tp")
+            hb = T[("hb", t)]
+            for gu in range(4):
+                g, u = divmod(gu, 2)
+                nc.tensor.transpose(tp[:, gu, :], hb[:].bitcast(F32)[:, 256 * g + u:256 * g + 256:2], idf[:, 0:P])
+            T[("hT", t)] = tp
+
+        def act_hg(t):
+            if not ok(t):
+                return
+            hg = p2.tile([P, C], BF16, name="hg", tag="hg", align_bytes=64)
+            nc.scalar.copy(out=hg[:].bitcast(F32).rearrange("p (g r u) -> p g r u", g=2, u=2),
+                           in_=T[("hT", t)][:].rearrange("p (g u) r -> p g r u", g=2))
+            T[("hg", t)] = hg
+
+        def pool_hf(t):
+            if not ok(t):
+                return
+            hf = hfp.tile([P, C], F32, name="hf", tag="hf")
+            nc.scalar.copy(out=hf[:], in_=T[("hb", t)][:])
+            T[("hf", t)] = hf
+
+        def dve_qh(t):
+            if not ok(t):
+                return
+            hq = p3.tile([P, 256], U32, name="hq", tag="hq", align_bytes=64)
+            hs = p3.tile([P, 256], U8, name="hs", tag="hs", align_bytes=64)
+            nc.vector.quantize_mx(out=hq[:].bitcast(FP8X4), scales=hs[:], in_=T[("hg", t)][:])
+            T[("hq", t)] = (hq, hs)
+
+        def pe_mm1(t):
+            if not ok(t):
+                return
+            hq, hs = T[("hq", t)]
+            z = ps_z.tile([P, 512], F32, name="z", tag="z")
+            for g in range(2):
+                nc.tensor.matmul_mx(out=z[:], lhsT=hq[:, P * g:P * g + P].bitcast(FP8X4), lhsT_scale=hs[:, P * g:P * g + P],
+                                    rhs=wwq[:, g, :].bitcast(FP8X4), rhs_scale=wws[:, g, :], start=(g == 0), stop=(g == 1))
+            T[("z", t)] = z
+
+        def dve_sm1(t):
+            if not ok(t):
+                return
+            zb = p2.tile([P, H, K], F32, name="zb", tag="zb")
+            nc.vector.tensor_tensor(out=zb[:].rearrange("p n k -> p (n k)"), in0=T[("z", t)][:], in1=bw_bc[:], op=ALU.add)
+            mx = p2.tile([P, H], F32, name="mx", tag="mx")
+            nc.vector.tensor_reduce(out=mx[:], in_=zb[:], axis=AX.X, op=ALU.max)
+            nc.vector.tensor_tensor(out=zb[:], in0=zb[:], in1=mx[:].unsqueeze(2).to_broadcast([P, H, K]), op=ALU.subtract)
+            T[("zb", t)] = zb
+
+        def act_exp(t):
+            if not ok(t):
+                return
+            ex = p2.tile([P, H, K], F32, name="ex", tag="ex")
+            nc.scalar.activation(out=ex[:], in_=T[("zb", t)][:], func=ACT.Exp)
+            T[("ex", t)] = ex
+
+        def dve_sm2(t):
+            if not ok(t):
+                return
+            ex = T[("ex", t)]
+            sums = p2.tile([P, H], F32, name="sums", tag="sums")
+            nc.vector.tensor_reduce(out=sums[:], in_=ex[:], axis=AX.X, op=ALU.add)
+            rs = p2.tile([P, H], F32, name="rs", tag="rs")
+            nc.vector.reciprocal(out=rs[:], in_=sums[:])
+            sv = stages[t % 3][:, 0:H * CH].rearrange("p (n c) -> p n c", c=CH)
+            nc.vector.tensor_tensor(out=sv[:, :, 0:K], in0=ex[:], in1=rs[:].unsqueeze(2).to_broadcast([P, H, K]), op=ALU.mult)
+
+        def sp_write(t):
+            if not ok(t):
+                return
+            nc.sync.dma_start(out=flat[t * 131072:(t + 1) * 131072].rearrange("(p w) -> p w", w=1024), in_=stages[t % 3][:])
+
+        def sp_reads(t):
+            if not ok(t):
+                return
+            bt = bands[t % NBAND]
+            ct = corners[t % NBAND]
+            for a in range(4):
+                base = t * 131072 + a * 32 * 1024
+                src = flat[base:base + 32 * 1023].rearrange("(i w) -> i w", w=1023)[:, 0:H * CH].rearrange("i (n c) -> i n c", c=CH)
+                if a == 0:
+                    if t >= NB:
+                        for j in range(4):
+                            nc.sync.dma_start(out=ct[32 * j:32 * j + 32, :, 32 * j + 1:32 * j + 32], in_=src[:, 4 * j:4 * j + 4, 0:31])
+                    nc.sync.dma_start(out=bt[0:32, :, 0:32], in_=src[:, :, 31:63])
+                else:
+                    nc.sync.dma_start(out=bt[32 * a:32 * a + 32, :, 32 * (a - 1) + 1:32 * (a - 1) + 64], in_=src[:, :, 0:63])
+
+        def pe_cornerT(t):
+            if not ok(t) or t < NB:
+                return
+            tp = ps_t.tile([P, 4, P], F32, name="tp", tag="tp")
+            for q in range(4):
+                nc.tensor.transpose(tp[:, q, :], corners[t % NBAND][:, q, :], idf[:, 0:P])
+            T[("lcT", t)] = tp
+
+        def act_lc(t):
+            if not ok(t) or t < NB:
+                return
+            lc = p2.tile([P, 4, P], F32, name="lc", tag="lc")
+            nc.scalar.copy(out=lc[:], in_=T[("lcT", t)][:])
+            T[("lc", t)] = lc
+
+        def pool_hcf(t):
+            if not ok(t) or t < NB:
+                return
+            hcf = p2.tile([P, 256], F32, name="hcf", tag="hcf")
+            nc.scalar.copy(out=hcf[:], in_=T[("hcb", t // NB)][:, t % NB, :])
+            T[("hcf", t)] = hcf
+
+        def pe_cornermm(t):
+            if not ok(t) or t < NB:
+                return
+            yk = ps_t.tile([P, 256], F32, name="yk", tag="tp")
+            lc = T[("lc", t)]
+            hcf = T[("hcf", t)]
+            for q in range(4):
+                nc.tensor.matmul(out=yk[:, R * q:R * q + R], lhsT=lc[:, q, :], rhs=hcf[:, R * q:R * q + R], start=True, stop=True)
+            T[("yk", t)] = yk
+
+        def act_ysb(t):
+            if not ok(t) or t < NB:
+                return
+            ysb = p2.tile([P, 256], F32, name="ysb", tag="ysb")
+            nc.scalar.copy(out=ysb[:], in_=T[("yk", t)][:])
+            T[("ysb", t)] = ysb
+
+        def pe_bandT(t, j):
+            if not ok(t):
+                return
+            off = (P - 32 * j) % P
+            tp = ps_t.tile([P, 4, P], F32, name="tp", tag="tp")
+            for q in range(4):
+                nc.tensor.transpose(tp[:, q, :], bands[t % NBAND][:, 4 * j + q, :], idf[:, off:off + P])
+            T[("ltT", t, j)] = tp
+
+        def act_lt(t, j):
+            if not ok(t):
+                return
+            if j == 0:
+                T[("lt", t)] = p2.tile([P, H, P], F32, name="lt", tag="lt")
+            nc.scalar.copy(out=T[("lt", t)][:, 4 * j:4 * j + 4, :], in_=T[("ltT", t, j)][:])
+
+        def pe_mm(t, j):
+            if not ok(t):
+                return
+            if j % 2 == 0:
+                T[("cd", t, j // 2)] = ps_c.tile([P, 512], F32, name="cd", tag="cd")
+            cd = T[("cd", t, j // 2)]
+            lt = T[("lt", t)]
+            hf = T[("hf", t)]
+            for q in range(4):
+                n = 4 * j + q
+                m = n % 8
+                nc.tensor.matmul(out=cd[:, R * m:R * m + R], lhsT=lt[:, n, :], rhs=hf[:, R * n:R * n + R], start=True, stop=True)
+
+        def dve_c(t, half):
+            if not ok(t):
+                return
+            if half == 0:
+                T[("cb", t)] = p2.tile([P, C], BF16, name="cb", tag="cb")
+            cb = T[("cb", t)]
+            cd = T[("cd", t, half)]
+            if t < NB:
+                nc.vector.tensor_copy(out=cb[:, 512 * half:512 * half + 512], in_=cd[:])
+            else:
+                for j in (2 * half, 2 * half + 1):
+                    nc.vector.scalar_tensor_tensor(out=cb[:, 256 * j:256 * j + 256], in0=T[("ysb", t)][:], scalar=msk[:, j:j + 1],
+                                                   in1=cd[:, 256 * (j % 2):256 * (j % 2) + 256], op0=ALU.mult, op1=ALU.add)
+
+        def pe_cT(t):
+            if not ok(t):
+                return
+            cb = T[("cb", t)]
+            for g in range(2):
+                tpb = ps_t.tile([P, 2, 4, P], BF16, name="tpb", tag="tp")
+                for v in range(2):
+                    j = 2 * g + v
+                    for tt in range(4):
+                        nc.tensor.transpose(tpb[:, v, tt, :], cb[:, 512 * g + tt:512 * g + 512:4], idb[:, 32 * j:32 * j + P])
+                T[("cT", t, g)] = tpb
+
+        def act_cg(t):
+            if not ok(t):
+                return
+            cg = p2.tile([P, C], BF16, name="cg", tag="cg", align_bytes=64)
+            for g in range(2):
+                for v in range(2):
+                    nc.scalar.copy(out=cg[64 * v:64 * v + 64, 512 * g:512 * g + 512].rearrange("p (r t) -> p r t", t=4),
+                                   in_=T[("cT", t, g)][64 * v:64 * v + 64, v, :, :].rearrange("p t r -> p r t"))
+            T[("cg", t)] = cg
+
+        def dve_qc(t):
+            if not ok(t):
+                return
+            cq = p2.tile([P, 256], U32, name="cq", tag="cq", align_bytes=64)
+            cs = p2.tile([P, 256], U8, name="cs", tag="cs", align_bytes=64)
+            nc.vector.quantize_mx(out=cq[:].bitcast(FP8X4), scales=cs[:], in_=T[("cg", t)][:])
+            T[("cq", t)] = (cq, cs)
+
+        def pe_mm2(t):
+            if not ok(t):
+                return
+            cq, cs = T[("cq", t)]
+            for e2 in range(2):
+                yp = ps_y.tile([P, 512], F32, name="yp", tag="yp")
+                for g in range(2):
+                    nc.tensor.matmul_mx(out=yp[:], lhsT=cq[:, P * g:P * g + P].bitcast(FP8X4), lhsT_scale=cs[:, P * g:P * g + P],
+                                        rhs=w2q[:, g, 512 * e2:512 * e2 + 512].bitcast(FP8X4), rhs_scale=w2s[:, g, 512 * e2:512 * e2 + 512],
+                                        start=(g == 0), stop=(g == 1))
+                T[("yp", t, e2)] = yp
+
+        def pool_xb(t):
+            if not ok(t):
+                return
+            xb = p3.tile([P, C], F32, name="xb", tag="xb")
+            nc.vector.tensor_tensor(out=xb[:], in0=T[("xt", t)][:], in1=b2_bc[:], op=ALU.add)
+            T[("xb", t)] = xb
+
+        def dve_v(t):
+            if not ok(t):
+                return
+            v = p2.tile([P, C], F32, name="v", tag="v")
+            s2 = p2.tile([P, 2], F32, name="s2", tag="s2")
+            xb = T[("xb", t)]
+            for e2 in range(2):
+                nc.vector.scalar_tensor_tensor(out=v[:, 512 * e2:512 * e2 + 512], in0=T[("yp", t, e2)][:], scalar=1.0,
+                                               in1=xb[:, 512 * e2:512 * e2 + 512], op0=ALU.mult, op1=ALU.add, accum_out=s2[:, e2:e2 + 1])
+            nm = p2.tile([P, 1], F32, name="nm", tag="nm")
+            nc.vector.tensor_scalar(out=nm[:], in0=s2[:, 0:1], scalar1=s2[:, 1:2], scalar2=-1.0 / C, op0=ALU.add, op1=ALU.mult)
+            T[("v", t)] = v
+            T[("nm", t)] = nm
+
+        def act_sq(t):
+            if not ok(t):
+                return
+            junk = p1.tile([P, C], BF16, name="junk", tag="junk")
+            ss = p2.tile([P, 1], F32, name="ss", tag="ss")
+            nc.scalar.activation(out=junk[:], in_=T[("v", t)][:], func=ACT.Square, bias=T[("nm", t)][:], scale=1.0, accum_out=ss[:])
+            T[("ss", t)] = ss
+
+        def pool_rstd(t):
+            if not ok(t):
+                return
+            ve = p2.tile([P, 1], F32, name="ve", tag="ve")
+            nc.gpsimd.tensor_scalar(out=ve[:], in0=T[("ss", t)][:], scalar1=1.0 / C, scalar2=EPS, op0=ALU.mult, op1=ALU.add)
+            rstd = p2.tile([P, 1], F32, name="rstd", tag="rstd")
+            nc.gpsimd.tensor_tensor(out=rstd[:], in0=ve[:], in1=nhalf[:], op=ALU.pow)
+            T[("rstd", t)] = rstd
+
+        def dve_A(t):
+            if not ok(t):
+                return
+            t1 = p2.tile([P, C], F32, name="t1", tag="t1")
+            nc.vector.scalar_tensor_tensor(out=t1[:], in0=T[("v", t)][:], scalar=T[("nm", t)][:], in1=g_bc[:], op0=ALU.add, op1=ALU.mult)
+            T[("t1", t)] = t1
+
+        def dve_B(t):
+            if not ok(t):
+                return
+            t1 = T[("t1", t)]
+            nc.vector.scalar_tensor_tensor(out=t1[:], in0=t1[:], scalar=T[("rstd", t)][:], in1=be_bc[:], op0=ALU.mult, op1=ALU.add)
+
+        def sp_store(t):
+            if not ok(t):
+                return
+            nc.sync.dma_start(out=out[P * (t // NB):P * (t // NB) + P, t % NB, :], in_=T[("t1", t)][:])
+
+        def w2_load(rt):
+            raw = wst.tile([P, C], BF16, name="raw", tag="raw")
+            nc.sync.dma_start(out=raw[:], in_=w2[P * rt:P * rt + P, :])
+            T[("raw", rt)] = raw
+
+        def w2_prep(rt):
+            tpb = ps_t.tile([P, 8, P], BF16, name="tpb", tag="tp")
+            raw = T[("raw", rt)]
+            for gt in range(8):
+                g, tt = divmod(gt, 4)
+                nc.tensor.transpose(tpb[:, gt, :], raw[:, 512 * g + tt:512 * g + 512:4], idb[:, 0:P])
+            nc.scalar.copy(out=gw2v[:, :, P * rt:P * rt + P, :], in_=tpb[:].rearrange("p (g t) r -> p g r t", g=2))
+
+        for s in range(NT + 8):
+            ld(s + 1)
+            if 1 - 1 <= s < 1 + 3:
+                w2_load(2 * (s - 1 + 1))
+                w2_load(2 * (s - 1 + 1) + 1)
+            if s == 1:
+                nc.sync.dma_start(out=b2_bc[:], in_=b2.partition_broadcast(P))
+            if s == 2:
+                nc.sync.dma_start(out=g_bc[:], in_=gamma.partition_broadcast(P))
+                nc.sync.dma_start(out=be_bc[:], in_=beta.partition_broadcast(P))
+            ld_x(s - 3)
+            if (s - 3) % NB == 0 and NB <= s - 3 < NT:
+                ld_hc((s - 3) // NB)
+            sp_reads(s - 3)
+
+            pe_mm(s - 5, 0)
+            pe_cT(s - 6)
+            dve_v(s - 7)
+            act_cg(s - 6)
+            pe_mm(s - 5, 1)
+            pe_hT(s)
+            act_hg(s)
+            pe_cornerT(s - 4)
+            act_lc(s - 4)
+            dve_sm1(s - 2)
+            dve_qc(s - 6)
+            pe_cornermm(s - 5)
+            act_ysb(s - 5)
+            act_sq(s - 7)
+            pe_bandT(s - 4, 0)
+            act_lt(s - 4, 0)
+            dve_A(s - 7)
+            pool_xb(s - 5)
+            pe_bandT(s - 4, 1)
+            act_lt(s - 4, 1)
+            act_exp(s - 2)
+            dve_c(s - 5, 0)
+            dve_qh(s)
+            pool_rstd(s - 7)
+            pe_mm(s - 5, 2)
+            dve_sm2(s - 2)
+            sp_write(s - 2)
+            pe_bandT(s - 4, 2)
+            act_lt(s - 4, 2)
+            pe_bandT(s - 4, 3)
+            act_lt(s - 4, 3)
+            pe_mm(s - 5, 3)
+            dve_B(s - 7)
+            sp_store(s - 7)
+            pool_hf(s)
+            pool_hcf(s - 4)
+            pe_mm1(s - 1)
+            pe_mm2(s - 6)
+            dve_c(s - 5, 1)
+            if 1 <= s < 1 + 4:
+                w2_prep(2 * (s - 1))
+                w2_prep(2 * (s - 1) + 1)
+            if 2 <= s < 4:
+                nc.vector.memset(bands[s - 1][:], 0.0)
+            if s == 4:
+                for ct in corners:
+                    nc.vector.memset(ct[:], 0.0)
+            if s == 1 + 4:
+                for g in range(2):
+                    nc.vector.quantize_mx(out=w2q[:, g, :].bitcast(FP8X4), scales=w2s[:, g, :], in_=gw2[:, 4096 * g:4096 * g + 4096])

@@ -24,7 +24,7 @@ R = 64
 CH = 63
 EPS = 1e-5
 NBAND = 3
-PINNED = True
+LAG = 11
 
 
 def tile_dynamicconvdecoderlayer_pa_kernel(tc, h, x, ww, bw, w2, b2, gamma, beta, out):
@@ -34,14 +34,12 @@ def tile_dynamicconvdecoderlayer_pa_kernel(tc, h, x, ww, bw, w2, b2, gamma, beta
         wst = ctx.enter_context(tc.tile_pool(name="wst", bufs=4))
         p2 = ctx.enter_context(tc.tile_pool(name="p2", bufs=2))
         p3 = ctx.enter_context(tc.tile_pool(name="p3", bufs=3))
-        hfp = ctx.enter_context(tc.tile_pool(name="hfp", bufs=7))
         p1 = ctx.enter_context(tc.tile_pool(name="p1", bufs=1))
         ps_t = ctx.enter_context(tc.psum_pool(name="ps_t", bufs=3))
         ps_z = ctx.enter_context(tc.psum_pool(name="ps_z", bufs=1))
         ps_c = ctx.enter_context(tc.psum_pool(name="ps_c", bufs=2))
         ps_y = ctx.enter_context(tc.psum_pool(name="ps_y", bufs=2))
-        if PINNED:
-            ctx.enter_context(tc.manual_schedule())
+        ctx.enter_context(tc.manual_schedule())
 
         flat = out.rearrange("t b e -> (t b e)")
         T = {}
@@ -49,37 +47,14 @@ def tile_dynamicconvdecoderlayer_pa_kernel(tc, h, x, ww, bw, w2, b2, gamma, beta
         def ok(t):
             return 0 <= t < NT
 
-        idf = const.tile([P, 2 * P], F32, name="idf")
-        make_identity(nc, idf[:, 0:P])
-        nc.vector.tensor_copy(out=idf[:, P:2 * P], in_=idf[:, 0:P])
-        idb = const.tile([P, 2 * P], BF16, name="idb")
-        nc.vector.tensor_copy(out=idb[:], in_=idf[:])
-        msk = const.tile([P, 4], F32, name="msk")
-        nc.vector.tensor_reduce(out=msk[:], in_=idf[:, 0:P].rearrange("p (j c) -> p j c", c=32), axis=AX.X, op=ALU.add)
-        nhalf = const.tile([P, 1], F32, name="nhalf")
-        nc.vector.memset(nhalf[:], -0.5)
+        hbs = [const.tile([P, C], BF16, name="hb%d" % i) for i in range(NT)]
         bw_bc = const.tile([P, H * K], BF16, name="bw_bc")
         b2_bc = const.tile([P, C], BF16, name="b2_bc")
         g_bc = const.tile([P, C], BF16, name="g_bc")
         be_bc = const.tile([P, C], BF16, name="be_bc")
-        wwq = const.tile([P, 2, 512], U32, name="wwq", align_bytes=64)
-        wws = const.tile([P, 2, 512], U8, name="wws", align_bytes=64)
-        w2q = const.tile([P, 2, 1024], U32, name="w2q", align_bytes=64)
-        w2s = const.tile([P, 2, 1024], U8, name="w2s", align_bytes=64)
-        gww = const.tile([P, 4096], BF16, name="gww", align_bytes=64)
-        gww32 = gww[:].bitcast(F32).rearrange("p (g c u) -> p g c u", g=2, u=2)
-        gw2 = const.tile([P, 8192], BF16, name="gw2", align_bytes=64)
-        gw2v = gw2[:].rearrange("p (g c t) -> p g c t", g=2, t=4)
-        stages = [const.tile([P, 1024], F32, name="stage%d" % i) for i in range(3)]
-        bands = [const.tile([P, H, P], F32, name="band%d" % i) for i in range(NBAND)]
-        corners = [const.tile([P, 4, P], F32, name="corner%d" % i) for i in range(NBAND)]
 
         def ld(t):
-            if not ok(t):
-                return
-            hb = p3.tile([P, C], BF16, name="hb", tag="hb")
-            nc.sync.dma_start(out=hb[:], in_=h[P * (t // NB):P * (t // NB) + P, t % NB, :])
-            T[("hb", t)] = hb
+            nc.sync.dma_start(out=hbs[t][:], in_=h[P * (t // NB):P * (t // NB) + P, t % NB, :])
 
         def ld_x(t):
             if not ok(t):
@@ -89,9 +64,9 @@ def tile_dynamicconvdecoderlayer_pa_kernel(tc, h, x, ww, bw, w2, b2, gamma, beta
             T[("xt", t)] = xt
 
         def ld_hc(ib):
-            hcb = p2.tile([P, NB, 256], BF16, name="hcb", tag="hcb")
-            for j in range(4):
-                nc.sync.dma_start(out=hcb[32 * j:32 * j + 32, :, :], in_=h[P * ib - 32:P * ib, :, 256 * j:256 * j + 256])
+            hcb = p1.tile([P, C], BF16, name="hcb", tag="hcb")
+            for b in range(NB):
+                nc.sync.dma_start(out=hcb[32 * b:32 * b + 32, :], in_=h[P * ib - 32:P * ib, b, :])
             T[("hcb", ib)] = hcb
 
         raws = []
@@ -101,8 +76,33 @@ def tile_dynamicconvdecoderlayer_pa_kernel(tc, h, x, ww, bw, w2, b2, gamma, beta
             raws.append(raw)
         ld(0)
         nc.sync.dma_start(out=bw_bc[:], in_=bw.partition_broadcast(P))
+        for t in range(1, 4):
+            ld(t)
+
+        idf = const.tile([P, 2 * P], F32, name="idf")
+        make_identity(nc, idf[:, 0:P])
+        nc.vector.tensor_copy(out=idf[:, P:2 * P], in_=idf[:, 0:P])
+        idb = const.tile([P, 2 * P], BF16, name="idb")
+        nc.vector.tensor_copy(out=idb[:], in_=idf[:])
+        msk = const.tile([P, 4], F32, name="msk")
+        nc.vector.tensor_reduce(out=msk[:], in_=idf[:, 0:P].rearrange("p (j c) -> p j c", c=32), axis=AX.X, op=ALU.add)
+        nhalf = const.tile([P, 1], F32, name="nhalf")
+        nc.gpsimd.memset(nhalf[:], -0.5)
+        wwq = const.tile([P, 2, 512], U32, name="wwq", align_bytes=64)
+        wws = const.tile([P, 2, 512], U8, name="wws", align_bytes=64)
+        w2q = const.tile([P, 2, 1024], U32, name="w2q", align_bytes=64)
+        w2s = const.tile([P, 2, 1024], U8, name="w2s", align_bytes=64)
+        stages = [const.tile([P, 1024], F32, name="stage%d" % i) for i in range(3)]
+        bands = [const.tile([P, H, P], F32, name="band%d" % i) for i in range(NBAND)]
+        corner = const.tile([P, H, P], F32, name="corner")
         for st in stages:
             nc.vector.memset(st[:], 0.0)
+        for bt in bands:
+            nc.gpsimd.memset(bt[:], 0.0)
+        nc.gpsimd.memset(corner[:], 0.0)
+
+        gww = p2.tile([P, 4096], BF16, name="gww", tag="lt", align_bytes=64)
+        gww32 = gww[:].bitcast(F32).rearrange("p (g c u) -> p g c u", g=2, u=2)
         for rt in range(4):
             tp = ps_t.tile([P, 4, P], F32, name="tp", tag="tp")
             for gu in range(4):
@@ -114,16 +114,14 @@ def tile_dynamicconvdecoderlayer_pa_kernel(tc, h, x, ww, bw, w2, b2, gamma, beta
                 nc.scalar.copy(out=gww32[:, :, P * rt:P * rt + P, :], in_=tp[:].rearrange("p (g u) r -> p g r u", g=2))
         for g in range(2):
             nc.vector.quantize_mx(out=wwq[:, g, :].bitcast(FP8X4), scales=wws[:, g, :], in_=gww[:, 2048 * g:2048 * g + 2048])
-        nc.vector.memset(bands[0][:], 0.0)
 
         def pe_hT(t):
             if not ok(t):
                 return
             tp = ps_t.tile([P, 4, P], F32, name="tp", tag="tp")
-            hb = T[("hb", t)]
             for gu in range(4):
                 g, u = divmod(gu, 2)
-                nc.tensor.transpose(tp[:, gu, :], hb[:].bitcast(F32)[:, 256 * g + u:256 * g + 256:2], idf[:, 0:P])
+                nc.tensor.transpose(tp[:, gu, :], hbs[t][:].bitcast(F32)[:, 256 * g + u:256 * g + 256:2], idf[:, 0:P])
             T[("hT", t)] = tp
 
         def act_hg(t):
@@ -134,11 +132,11 @@ def tile_dynamicconvdecoderlayer_pa_kernel(tc, h, x, ww, bw, w2, b2, gamma, beta
                            in_=T[("hT", t)][:].rearrange("p (g u) r -> p g r u", g=2))
             T[("hg", t)] = hg
 
-        def pool_hf(t):
+        def act_hf(t):
             if not ok(t):
                 return
-            hf = hfp.tile([P, C], F32, name="hf", tag="hf")
-            nc.scalar.copy(out=hf[:], in_=T[("hb", t)][:])
+            hf = p2.tile([P, C], F32, name="hf", tag="hf")
+            nc.scalar.copy(out=hf[:].rearrange("p (n t q) -> p n t q", t=4, q=16), in_=hbs[t][:].rearrange("p (n q t) -> p n t q", t=4, q=16))
             T[("hf", t)] = hf
 
         def dve_qh(t):
@@ -159,15 +157,25 @@ def tile_dynamicconvdecoderlayer_pa_kernel(tc, h, x, ww, bw, w2, b2, gamma, beta
                                     rhs=wwq[:, g, :].bitcast(FP8X4), rhs_scale=wws[:, g, :], start=(g == 0), stop=(g == 1))
             T[("z", t)] = z
 
-        def dve_sm1(t):
+        def dve_zb(t):
             if not ok(t):
                 return
             zb = p2.tile([P, H, K], F32, name="zb", tag="zb")
             nc.vector.tensor_tensor(out=zb[:].rearrange("p n k -> p (n k)"), in0=T[("z", t)][:], in1=bw_bc[:], op=ALU.add)
-            mx = p2.tile([P, H], F32, name="mx", tag="mx")
-            nc.vector.tensor_reduce(out=mx[:], in_=zb[:], axis=AX.X, op=ALU.max)
-            nc.vector.tensor_tensor(out=zb[:], in0=zb[:], in1=mx[:].unsqueeze(2).to_broadcast([P, H, K]), op=ALU.subtract)
             T[("zb", t)] = zb
+
+        def dve_max(t):
+            if not ok(t):
+                return
+            mx = p2.tile([P, H], F32, name="mx", tag="mx")
+            nc.vector.tensor_reduce(out=mx[:], in_=T[("zb", t)][:], axis=AX.X, op=ALU.max)
+            T[("mx", t)] = mx
+
+        def dve_sub(t):
+            if not ok(t):
+                return
+            zb = T[("zb", t)]
+            nc.vector.tensor_tensor(out=zb[:], in0=zb[:], in1=T[("mx", t)][:].unsqueeze(2).to_broadcast([P, H, K]), op=ALU.subtract)
 
         def act_exp(t):
             if not ok(t):
@@ -176,81 +184,81 @@ def tile_dynamicconvdecoderlayer_pa_kernel(tc, h, x, ww, bw, w2, b2, gamma, beta
             nc.scalar.activation(out=ex[:], in_=T[("zb", t)][:], func=ACT.Exp)
             T[("ex", t)] = ex
 
-        def dve_sm2(t):
+        def dve_sum(t):
             if not ok(t):
                 return
-            ex = T[("ex", t)]
             sums = p2.tile([P, H], F32, name="sums", tag="sums")
-            nc.vector.tensor_reduce(out=sums[:], in_=ex[:], axis=AX.X, op=ALU.add)
+            nc.vector.tensor_reduce(out=sums[:], in_=T[("ex", t)][:], axis=AX.X, op=ALU.add)
+            T[("sums", t)] = sums
+
+        def dve_rs(t):
+            if not ok(t):
+                return
             rs = p2.tile([P, H], F32, name="rs", tag="rs")
-            nc.vector.reciprocal(out=rs[:], in_=sums[:])
+            nc.vector.reciprocal(out=rs[:], in_=T[("sums", t)][:])
+            T[("rs", t)] = rs
+
+        def dve_w(t):
+            if not ok(t):
+                return
             sv = stages[t % 3][:, 0:H * CH].rearrange("p (n c) -> p n c", c=CH)
-            nc.vector.tensor_tensor(out=sv[:, :, 0:K], in0=ex[:], in1=rs[:].unsqueeze(2).to_broadcast([P, H, K]), op=ALU.mult)
+            nc.vector.tensor_tensor(out=sv[:, :, 0:K], in0=T[("ex", t)][:], in1=T[("rs", t)][:].unsqueeze(2).to_broadcast([P, H, K]), op=ALU.mult)
 
         def sp_write(t):
             if not ok(t):
                 return
             nc.sync.dma_start(out=flat[t * 131072:(t + 1) * 131072].rearrange("(p w) -> p w", w=1024), in_=stages[t % 3][:])
 
+        def skewed(t, a):
+            base = t * 131072 + a * 32 * 1024
+            return flat[base:base + 32 * 1023].rearrange("(i w) -> i w", w=1023)[:, 0:H * CH].rearrange("i (n c) -> i n c", c=CH)
+
         def sp_reads(t):
             if not ok(t):
                 return
             bt = bands[t % NBAND]
-            ct = corners[t % NBAND]
-            for a in range(4):
-                base = t * 131072 + a * 32 * 1024
-                src = flat[base:base + 32 * 1023].rearrange("(i w) -> i w", w=1023)[:, 0:H * CH].rearrange("i (n c) -> i n c", c=CH)
-                if a == 0:
-                    if t >= NB:
-                        for j in range(4):
-                            nc.sync.dma_start(out=ct[32 * j:32 * j + 32, :, 32 * j + 1:32 * j + 32], in_=src[:, 4 * j:4 * j + 4, 0:31])
-                    nc.sync.dma_start(out=bt[0:32, :, 0:32], in_=src[:, :, 31:63])
-                else:
-                    nc.sync.dma_start(out=bt[32 * a:32 * a + 32, :, 32 * (a - 1) + 1:32 * (a - 1) + 64], in_=src[:, :, 0:63])
+            nc.sync.dma_start(out=bt[0:32, :, 0:32], in_=skewed(t, 0)[:, :, 31:63])
+            for a in range(1, 4):
+                nc.sync.dma_start(out=bt[32 * a:32 * a + 32, :, 32 * (a - 1) + 1:32 * (a - 1) + 64], in_=skewed(t, a))
 
-        def pe_cornerT(t):
-            if not ok(t) or t < NB:
-                return
+        def sp_corner(ib, b):
+            nc.sync.dma_start(out=corner[32 * b:32 * b + 32, :, 32 * b + 1:32 * b + 32], in_=skewed(NB * ib + b, 0)[:, :, 0:31])
+
+        def pe_cornerT(ib, j):
             tp = ps_t.tile([P, 4, P], F32, name="tp", tag="tp")
             for q in range(4):
-                nc.tensor.transpose(tp[:, q, :], corners[t % NBAND][:, q, :], idf[:, 0:P])
-            T[("lcT", t)] = tp
+                nc.tensor.transpose(tp[:, q, :], corner[:, 4 * j + q, :], idf[:, 0:P])
+            T[("lcT", ib, j)] = tp
 
-        def act_lc(t):
-            if not ok(t) or t < NB:
-                return
+        def act_lc(ib, j):
             lc = p2.tile([P, 4, P], F32, name="lc", tag="lc")
-            nc.scalar.copy(out=lc[:], in_=T[("lcT", t)][:])
-            T[("lc", t)] = lc
+            nc.scalar.copy(out=lc[:], in_=T[("lcT", ib, j)][:])
+            T[("lc", ib, j)] = lc
 
-        def pool_hcf(t):
-            if not ok(t) or t < NB:
-                return
-            hcf = p2.tile([P, 256], F32, name="hcf", tag="hcf")
-            nc.scalar.copy(out=hcf[:], in_=T[("hcb", t // NB)][:, t % NB, :])
-            T[("hcf", t)] = hcf
+        def act_hcf(ib):
+            hcf = p2.tile([P, C], F32, name="hcf", tag="hcf")
+            nc.scalar.copy(out=hcf[:].rearrange("p (n t q) -> p n t q", t=4, q=16), in_=T[("hcb", ib)][:].rearrange("p (n q t) -> p n t q", t=4, q=16))
+            T[("hcf", ib)] = hcf
 
-        def pe_cornermm(t):
-            if not ok(t) or t < NB:
-                return
-            yk = ps_t.tile([P, 256], F32, name="yk", tag="tp")
-            lc = T[("lc", t)]
-            hcf = T[("hcf", t)]
+        def pe_cornermm(ib, j):
+            yk = ps_t.tile([P, 4, 4, 16], F32, name="yk", tag="tp")
+            lc = T[("lc", ib, j)]
+            hcf = T[("hcf", ib)]
             for q in range(4):
-                nc.tensor.matmul(out=yk[:, R * q:R * q + R], lhsT=lc[:, q, :], rhs=hcf[:, R * q:R * q + R], start=True, stop=True)
-            T[("yk", t)] = yk
+                n = 4 * j + q
+                nc.tensor.matmul(out=yk[:, :, q, :], lhsT=lc[:, q, :], rhs=hcf[:, R * n:R * n + R], start=True, stop=True)
+            T[("yk", ib, j)] = yk
 
-        def act_ysb(t):
-            if not ok(t) or t < NB:
-                return
-            ysb = p2.tile([P, 256], F32, name="ysb", tag="ysb")
-            nc.scalar.copy(out=ysb[:], in_=T[("yk", t)][:])
-            T[("ysb", t)] = ysb
+        def act_ysb(ib, j):
+            if j == 0:
+                T[("ysb", ib)] = p2.tile([P, C], F32, name="ysb", tag="ysb")
+            ysb = T[("ysb", ib)][:, 512 * (j // 2):512 * (j // 2) + 512].rearrange("p (t m q) -> p t (m q)", t=4, m=8)
+            nc.scalar.copy(out=ysb[:, :, 64 * (j % 2):64 * (j % 2) + 64], in_=T[("yk", ib, j)][:].rearrange("p t m q -> p t (m q)"))
 
         def pe_bandT(t, j):
             if not ok(t):
                 return
-            off = (P - 32 * j) % P
+            off = (P - 32 * (t % NB)) % P
             tp = ps_t.tile([P, 4, P], F32, name="tp", tag="tp")
             for q in range(4):
                 nc.tensor.transpose(tp[:, q, :], bands[t % NBAND][:, 4 * j + q, :], idf[:, off:off + P])
@@ -260,56 +268,49 @@ def tile_dynamicconvdecoderlayer_pa_kernel(tc, h, x, ww, bw, w2, b2, gamma, beta
             if not ok(t):
                 return
             if j == 0:
-                T[("lt", t)] = p2.tile([P, H, P], F32, name="lt", tag="lt")
+                T[("lt", t)] = p2.tile([P, H, P], F32, name="lt", tag="lt", align_bytes=64)
             nc.scalar.copy(out=T[("lt", t)][:, 4 * j:4 * j + 4, :], in_=T[("ltT", t, j)][:])
 
         def pe_mm(t, j):
             if not ok(t):
                 return
             if j % 2 == 0:
-                T[("cd", t, j // 2)] = ps_c.tile([P, 512], F32, name="cd", tag="cd")
+                T[("cd", t, j // 2)] = ps_c.tile([P, 4, 8, 16], F32, name="cd", tag="cd")
             cd = T[("cd", t, j // 2)]
             lt = T[("lt", t)]
             hf = T[("hf", t)]
             for q in range(4):
                 n = 4 * j + q
-                m = n % 8
-                nc.tensor.matmul(out=cd[:, R * m:R * m + R], lhsT=lt[:, n, :], rhs=hf[:, R * n:R * n + R], start=True, stop=True)
+                nc.tensor.matmul(out=cd[:, :, n % 8, :], lhsT=lt[:, n, :], rhs=hf[:, R * n:R * n + R], start=True, stop=True)
 
         def dve_c(t, half):
             if not ok(t):
                 return
             if half == 0:
                 T[("cb", t)] = p2.tile([P, C], BF16, name="cb", tag="cb")
-            cb = T[("cb", t)]
-            cd = T[("cd", t, half)]
+            cb = T[("cb", t)][:, 512 * half:512 * half + 512]
+            cd = T[("cd", t, half)][:].rearrange("p t m q -> p (t m q)")
             if t < NB:
-                nc.vector.tensor_copy(out=cb[:, 512 * half:512 * half + 512], in_=cd[:])
+                nc.vector.tensor_copy(out=cb, in_=cd)
             else:
-                for j in (2 * half, 2 * half + 1):
-                    nc.vector.scalar_tensor_tensor(out=cb[:, 256 * j:256 * j + 256], in0=T[("ysb", t)][:], scalar=msk[:, j:j + 1],
-                                                   in1=cd[:, 256 * (j % 2):256 * (j % 2) + 256], op0=ALU.mult, op1=ALU.add)
+                ysb = T[("ysb", t // NB)][:, 512 * half:512 * half + 512]
+                nc.vector.scalar_tensor_tensor(out=cb, in0=ysb, scalar=msk[:, t % NB:t % NB + 1], in1=cd, op0=ALU.mult, op1=ALU.add)
 
         def pe_cT(t):
             if not ok(t):
                 return
+            tpb = ps_t.tile([P, 8, P], BF16, name="tpb", tag="tp")
             cb = T[("cb", t)]
-            for g in range(2):
-                tpb = ps_t.tile([P, 2, 4, P], BF16, name="tpb", tag="tp")
-                for v in range(2):
-                    j = 2 * g + v
-                    for tt in range(4):
-                        nc.tensor.transpose(tpb[:, v, tt, :], cb[:, 512 * g + tt:512 * g + 512:4], idb[:, 32 * j:32 * j + P])
-                T[("cT", t, g)] = tpb
+            off = 32 * (t % NB)
+            for ch in range(8):
+                nc.tensor.transpose(tpb[:, ch, :], cb[:, P * ch:P * ch + P], idb[:, off:off + P])
+            T[("cT", t)] = tpb
 
         def act_cg(t):
             if not ok(t):
                 return
             cg = p2.tile([P, C], BF16, name="cg", tag="cg", align_bytes=64)
-            for g in range(2):
-                for v in range(2):
-                    nc.scalar.copy(out=cg[64 * v:64 * v + 64, 512 * g:512 * g + 512].rearrange("p (r t) -> p r t", t=4),
-                                   in_=T[("cT", t, g)][64 * v:64 * v + 64, v, :, :].rearrange("p t r -> p r t"))
+            nc.scalar.copy(out=cg[:].rearrange("p (g r t) -> p g r t", g=2, t=4), in_=T[("cT", t)][:].rearrange("p (g t) r -> p g r t", g=2))
             T[("cg", t)] = cg
 
         def dve_qc(t):
@@ -332,10 +333,10 @@ def tile_dynamicconvdecoderlayer_pa_kernel(tc, h, x, ww, bw, w2, b2, gamma, beta
                                         start=(g == 0), stop=(g == 1))
                 T[("yp", t, e2)] = yp
 
-        def pool_xb(t):
+        def dve_xb(t):
             if not ok(t):
                 return
-            xb = p3.tile([P, C], F32, name="xb", tag="xb")
+            xb = p2.tile([P, C], F32, name="xb", tag="xb")
             nc.vector.tensor_tensor(out=xb[:], in0=T[("xt", t)][:], in1=b2_bc[:], op=ALU.add)
             T[("xb", t)] = xb
 
@@ -348,9 +349,15 @@ def tile_dynamicconvdecoderlayer_pa_kernel(tc, h, x, ww, bw, w2, b2, gamma, beta
             for e2 in range(2):
                 nc.vector.scalar_tensor_tensor(out=v[:, 512 * e2:512 * e2 + 512], in0=T[("yp", t, e2)][:], scalar=1.0,
                                                in1=xb[:, 512 * e2:512 * e2 + 512], op0=ALU.mult, op1=ALU.add, accum_out=s2[:, e2:e2 + 1])
+            T[("v", t)] = v
+            T[("s2", t)] = s2
+
+        def dve_nm(t):
+            if not ok(t):
+                return
+            s2 = T[("s2", t)]
             nm = p2.tile([P, 1], F32, name="nm", tag="nm")
             nc.vector.tensor_scalar(out=nm[:], in0=s2[:, 0:1], scalar1=s2[:, 1:2], scalar2=-1.0 / C, op0=ALU.add, op1=ALU.mult)
-            T[("v", t)] = v
             T[("nm", t)] = nm
 
         def act_sq(t):
@@ -394,75 +401,92 @@ def tile_dynamicconvdecoderlayer_pa_kernel(tc, h, x, ww, bw, w2, b2, gamma, beta
             T[("raw", rt)] = raw
 
         def w2_prep(rt):
-            tpb = ps_t.tile([P, 8, P], BF16, name="tpb", tag="tp")
+            if rt == 0:
+                T["gw2"] = [p2.tile([P, 4096], BF16, name="gw2", tag="lt", align_bytes=64) for g in range(2)]
             raw = T[("raw", rt)]
+            tpb = ps_t.tile([P, 8, P], BF16, name="tpb", tag="tp")
             for gt in range(8):
-                g, tt = divmod(gt, 4)
-                nc.tensor.transpose(tpb[:, gt, :], raw[:, 512 * g + tt:512 * g + 512:4], idb[:, 0:P])
-            nc.scalar.copy(out=gw2v[:, :, P * rt:P * rt + P, :], in_=tpb[:].rearrange("p (g t) r -> p g r t", g=2))
+                g, t = divmod(gt, 4)
+                nc.tensor.transpose(tpb[:, gt, :], raw[:, 512 * g + t:512 * g + 512:4], idb[:, 0:P])
+            for g in range(2):
+                nc.scalar.copy(out=T["gw2"][g][:].rearrange("p (c t) -> p c t", t=4)[:, P * rt:P * rt + P, :],
+                               in_=tpb[:, 4 * g:4 * g + 4, :].rearrange("p t r -> p r t"))
 
-        for s in range(NT + 8):
-            ld(s + 1)
-            if 1 - 1 <= s < 1 + 3:
-                w2_load(2 * (s - 1 + 1))
-                w2_load(2 * (s - 1 + 1) + 1)
-            if s == 1:
-                nc.sync.dma_start(out=b2_bc[:], in_=b2.partition_broadcast(P))
+        for s in range(-2, NT + LAG + 4):
+            a, a1, a2 = s, s - 1, s - 2
+            b0, b1, b2t, b3 = s - LAG, s - LAG - 1, s - LAG - 2, s - LAG - 3
+            ct = [(ib, j) for ib in range(1, NI) for j in range(4) if s == 4 * ib + 7 + j // 1]
+            cm = [(ib, j) for ib in range(1, NI) for j in range(4) if s == 4 * ib + 8 + j // 1]
+            if 0 <= s < NT - 4:
+                ld(s + 4)
+            if 0 <= s < 4:
+                w2_load(2 * s)
+                w2_load(2 * s + 1)
             if s == 2:
+                nc.sync.dma_start(out=b2_bc[:], in_=b2.partition_broadcast(P))
+            if s == 3:
                 nc.sync.dma_start(out=g_bc[:], in_=gamma.partition_broadcast(P))
                 nc.sync.dma_start(out=be_bc[:], in_=beta.partition_broadcast(P))
-            ld_x(s - 3)
-            if (s - 3) % NB == 0 and NB <= s - 3 < NT:
-                ld_hc((s - 3) // NB)
-            sp_reads(s - 3)
+            ld_x(b0)
+            for ib in range(1, NI):
+                if s == 4 * ib + 5:
+                    ld_hc(ib)
+            sp_reads(b0 + 2)
 
-            pe_mm(s - 5, 0)
-            pe_cT(s - 6)
-            dve_v(s - 7)
-            act_cg(s - 6)
-            pe_mm(s - 5, 1)
-            pe_hT(s)
-            act_hg(s)
-            pe_cornerT(s - 4)
-            act_lc(s - 4)
-            dve_sm1(s - 2)
-            dve_qc(s - 6)
-            pe_cornermm(s - 5)
-            act_ysb(s - 5)
-            act_sq(s - 7)
-            pe_bandT(s - 4, 0)
-            act_lt(s - 4, 0)
-            dve_A(s - 7)
-            pool_xb(s - 5)
-            pe_bandT(s - 4, 1)
-            act_lt(s - 4, 1)
-            act_exp(s - 2)
-            dve_c(s - 5, 0)
-            dve_qh(s)
-            pool_rstd(s - 7)
-            pe_mm(s - 5, 2)
-            dve_sm2(s - 2)
-            sp_write(s - 2)
-            pe_bandT(s - 4, 2)
-            act_lt(s - 4, 2)
-            pe_bandT(s - 4, 3)
-            act_lt(s - 4, 3)
-            pe_mm(s - 5, 3)
-            dve_B(s - 7)
-            sp_store(s - 7)
-            pool_hf(s)
-            pool_hcf(s - 4)
-            pe_mm1(s - 1)
-            pe_mm2(s - 6)
-            dve_c(s - 5, 1)
-            if 1 <= s < 1 + 4:
+            act_lt(b0, 0)
+            dve_qc(b2t)
+            pe_bandT(b0, 1)
+            act_lt(b0, 1)
+            pe_mm2(b2t)
+            dve_qh(a)
+            dve_zb(a1)
+            pe_bandT(b0, 2)
+            act_lt(b0, 2)
+            dve_c(b1, 0)
+            dve_c(b1, 1)
+            dve_B(b3)
+            sp_store(b3)
+            pe_mm1(a)
+            pe_hT(a + 2)
+            act_hg(a + 2)
+            for ib, j in cm:
+                pe_cornermm(ib, j)
+                act_ysb(ib, j)
+            dve_max(a1)
+            dve_xb(b2t)
+            pe_cT(b1)
+            act_cg(b1)
+            dve_v(b2t)
+            dve_sum(a2)
+            dve_nm(b2t)
+            act_sq(b2t)
+            pool_rstd(b2t)
+            dve_sub(a1)
+            act_exp(a1)
+            pe_bandT(b0, 3)
+            act_lt(b0, 3)
+            act_hf(b0 + 1)
+            for ib, j in ct:
+                if j == 0:
+                    act_hcf(ib)
+                pe_cornerT(ib, j)
+                act_lc(ib, j)
+            dve_A(b2t)
+            dve_rs(a2)
+            dve_w(a2)
+            sp_write(a2)
+            pe_mm(b0, 0)
+            pe_mm(b0, 1)
+            pe_mm(b0, 2)
+            pe_mm(b0, 3)
+            pe_bandT(b0 + 1, 0)
+            if 1 <= s < 5:
                 w2_prep(2 * (s - 1))
                 w2_prep(2 * (s - 1) + 1)
-            if 2 <= s < 4:
-                nc.vector.memset(bands[s - 1][:], 0.0)
-            if s == 4:
-                for ct in corners:
-                    nc.vector.memset(ct[:], 0.0)
-            if s == 1 + 4:
+            if s == 5:
                 for g in range(2):
-                    nc.vector.quantize_mx(out=w2q[:, g, :].bitcast(FP8X4), scales=w2s[:, g, :], in_=gw2[:, 4096 * g:4096 * g + 4096])
+                    nc.vector.quantize_mx(out=w2q[:, g, :].bitcast(FP8X4), scales=w2s[:, g, :], in_=T["gw2"][g][:])
+            for ib in range(1, NI):
+                if s == 4 * ib + 6:
+                    for b in range(NB):
+                        sp_corner(ib, b)

@@ -21,10 +21,9 @@ C = 1024
 H = 16
 K = 32
 R = 64
-CH = 63
+SL = 64
 EPS = 1e-5
-NBAND = 3
-LAG = 11
+LAG = 8
 
 
 def tile_dynamicconvdecoderlayer_pa_kernel(tc, h, x, ww, bw, w2, b2, gamma, beta, out):
@@ -79,22 +78,22 @@ def tile_dynamicconvdecoderlayer_pa_kernel(tc, h, x, ww, bw, w2, b2, gamma, beta
         for t in range(1, 4):
             ld(t)
 
-        idf = const.tile([P, 2 * P], F32, name="idf")
-        make_identity(nc, idf[:, 0:P])
-        nc.vector.tensor_copy(out=idf[:, P:2 * P], in_=idf[:, 0:P])
+        idf = const.tile([P, P], F32, name="idf")
+        make_identity(nc, idf[:])
         idb = const.tile([P, 2 * P], BF16, name="idb")
-        nc.vector.tensor_copy(out=idb[:], in_=idf[:])
+        nc.vector.tensor_copy(out=idb[:, 0:P], in_=idf[:])
+        nc.vector.tensor_copy(out=idb[:, P:2 * P], in_=idf[:])
         msk = const.tile([P, 4], F32, name="msk")
-        nc.vector.tensor_reduce(out=msk[:], in_=idf[:, 0:P].rearrange("p (j c) -> p j c", c=32), axis=AX.X, op=ALU.add)
+        nc.vector.tensor_reduce(out=msk[:], in_=idf[:].rearrange("p (j c) -> p j c", c=32), axis=AX.X, op=ALU.add)
         nhalf = const.tile([P, 1], F32, name="nhalf")
         nc.gpsimd.memset(nhalf[:], -0.5)
         wwq = const.tile([P, 2, 512], U32, name="wwq", align_bytes=64)
         wws = const.tile([P, 2, 512], U8, name="wws", align_bytes=64)
         w2q = const.tile([P, 2, 1024], U32, name="w2q", align_bytes=64)
         w2s = const.tile([P, 2, 1024], U8, name="w2s", align_bytes=64)
-        stages = [const.tile([P, 1024], F32, name="stage%d" % i) for i in range(3)]
-        bands = [const.tile([P, H, P], F32, name="band%d" % i) for i in range(NBAND)]
-        corner = const.tile([P, H, P], F32, name="corner")
+        stages = [const.tile([P, SL, 2, H], F32, name="stage%d" % i) for i in range(2)]
+        bands = [const.tile([P, P, 2 * H], F32, name="band%d" % i) for i in range(2)]
+        corner = const.tile([P, P, H], F32, name="corner")
         for st in stages:
             nc.vector.memset(st[:], 0.0)
         for bt in bands:
@@ -107,7 +106,7 @@ def tile_dynamicconvdecoderlayer_pa_kernel(tc, h, x, ww, bw, w2, b2, gamma, beta
             tp = ps_t.tile([P, 4, P], F32, name="tp", tag="tp")
             for gu in range(4):
                 g, u = divmod(gu, 2)
-                nc.tensor.transpose(tp[:, gu, :], raws[rt][:].bitcast(F32)[:, 256 * g + u:256 * g + 256:2], idf[:, 0:P])
+                nc.tensor.transpose(tp[:, gu, :], raws[rt][:].bitcast(F32)[:, 256 * g + u:256 * g + 256:2], idf[:])
             if rt % 2 == 0:
                 nc.vector.tensor_copy(out=gww32[:, :, P * rt:P * rt + P, :], in_=tp[:].rearrange("p (g u) r -> p g r u", g=2))
             else:
@@ -121,7 +120,7 @@ def tile_dynamicconvdecoderlayer_pa_kernel(tc, h, x, ww, bw, w2, b2, gamma, beta
             tp = ps_t.tile([P, 4, P], F32, name="tp", tag="tp")
             for gu in range(4):
                 g, u = divmod(gu, 2)
-                nc.tensor.transpose(tp[:, gu, :], hbs[t][:].bitcast(F32)[:, 256 * g + u:256 * g + 256:2], idf[:, 0:P])
+                nc.tensor.transpose(tp[:, gu, :], hbs[t][:].bitcast(F32)[:, 256 * g + u:256 * g + 256:2], idf[:])
             T[("hT", t)] = tp
 
         def act_hg(t):
@@ -201,38 +200,32 @@ def tile_dynamicconvdecoderlayer_pa_kernel(tc, h, x, ww, bw, w2, b2, gamma, beta
         def dve_w(t):
             if not ok(t):
                 return
-            sv = stages[t % 3][:, 0:H * CH].rearrange("p (n c) -> p n c", c=CH)
-            nc.vector.tensor_tensor(out=sv[:, :, 0:K], in0=T[("ex", t)][:], in1=T[("rs", t)][:].unsqueeze(2).to_broadcast([P, H, K]), op=ALU.mult)
+            nc.vector.tensor_tensor(out=stages[t // 2 % 2][:, 1:1 + K, t % 2, :], in0=T[("ex", t)][:].rearrange("p n k -> p k n"),
+                                    in1=T[("rs", t)][:].unsqueeze(1).to_broadcast([P, K, H]), op=ALU.mult)
 
         def sp_write(t):
-            if not ok(t):
+            if not ok(t) or t % 2 == 0:
                 return
-            nc.sync.dma_start(out=flat[t * 131072:(t + 1) * 131072].rearrange("(p w) -> p w", w=1024), in_=stages[t % 3][:])
-
-        def skewed(t, a):
-            base = t * 131072 + a * 32 * 1024
-            return flat[base:base + 32 * 1023].rearrange("(i w) -> i w", w=1023)[:, 0:H * CH].rearrange("i (n c) -> i n c", c=CH)
+            base = t // 2 * 2 * 131072
+            nc.sync.dma_start(out=flat[base:base + 262144].rearrange("(p w) -> p w", w=2048), in_=stages[t // 2 % 2][:].rearrange("p k b n -> p (k b n)"))
 
         def sp_reads(t):
-            if not ok(t):
+            if not ok(t) or t % 2 == 1:
                 return
-            bt = bands[t % NBAND]
-            nc.sync.dma_start(out=bt[0:32, :, 0:32], in_=skewed(t, 0)[:, :, 31:63])
-            for a in range(1, 4):
-                nc.sync.dma_start(out=bt[32 * a:32 * a + 32, :, 32 * (a - 1) + 1:32 * (a - 1) + 64], in_=skewed(t, a))
+            for a in range(8):
+                ni = min(47, P - 16 * a)
+                base = t * 131072 + 16 * a * 2048 + 512
+                src = flat[base:base + ni * 2016].rearrange("(i w) -> i w", w=2016)[:, 512:1024].rearrange("i (s c) -> s i c", c=2 * H)
+                nc.sync.dma_start(out=bands[t // 2 % 2][16 * a:16 * a + 16, 16 * a:16 * a + ni, :], in_=src)
 
         def sp_corner(ib, b):
-            nc.sync.dma_start(out=corner[32 * b:32 * b + 32, :, 32 * b + 1:32 * b + 32], in_=skewed(NB * ib + b, 0)[:, :, 0:31])
-
-        def pe_cornerT(ib, j):
-            tp = ps_t.tile([P, 4, P], F32, name="tp", tag="tp")
-            for q in range(4):
-                nc.tensor.transpose(tp[:, q, :], corner[:, 4 * j + q, :], idf[:, 0:P])
-            T[("lcT", ib, j)] = tp
+            base = (NB * ib + b) // 2 * 2 * 131072
+            src = flat[base:base + 32 * 2016].rearrange("(i w) -> i w", w=2016)[:, 0:1024].rearrange("i (s c) -> s i c", c=2 * H)
+            nc.sync.dma_start(out=corner[32 * b:32 * b + 32, 32 * b:32 * b + 32, :], in_=src[:, :, H * (b % 2):H * (b % 2) + H])
 
         def act_lc(ib, j):
-            lc = p2.tile([P, 4, P], F32, name="lc", tag="lc")
-            nc.scalar.copy(out=lc[:], in_=T[("lcT", ib, j)][:])
+            lc = p2.tile([P, 4, P], F32, name="lc", tag="lc", bufs=4)
+            nc.scalar.copy(out=lc[:].rearrange("p n i -> p i n"), in_=corner[:, :, 4 * j:4 * j + 4])
             T[("lc", ib, j)] = lc
 
         def act_hcf(ib):
@@ -255,21 +248,17 @@ def tile_dynamicconvdecoderlayer_pa_kernel(tc, h, x, ww, bw, w2, b2, gamma, beta
             ysb = T[("ysb", ib)][:, 512 * (j // 2):512 * (j // 2) + 512].rearrange("p (t m q) -> p t (m q)", t=4, m=8)
             nc.scalar.copy(out=ysb[:, :, 64 * (j % 2):64 * (j % 2) + 64], in_=T[("yk", ib, j)][:].rearrange("p t m q -> p t (m q)"))
 
-        def pe_bandT(t, j):
-            if not ok(t):
-                return
-            off = (P - 32 * (t % NB)) % P
-            tp = ps_t.tile([P, 4, P], F32, name="tp", tag="tp")
-            for q in range(4):
-                nc.tensor.transpose(tp[:, q, :], bands[t % NBAND][:, 4 * j + q, :], idf[:, off:off + P])
-            T[("ltT", t, j)] = tp
-
         def act_lt(t, j):
             if not ok(t):
                 return
             if j == 0:
                 T[("lt", t)] = p2.tile([P, H, P], F32, name="lt", tag="lt", align_bytes=64)
-            nc.scalar.copy(out=T[("lt", t)][:, 4 * j:4 * j + 4, :], in_=T[("ltT", t, j)][:])
+            lt = T[("lt", t)][:, 4 * j:4 * j + 4, :].rearrange("p n i -> p i n")
+            src = bands[t // 2 % 2][:, :, H * (t % 2) + 4 * j:H * (t % 2) + 4 * j + 4]
+            turn = 32 * (t % NB)
+            nc.scalar.copy(out=lt[:, turn:P, :], in_=src[:, 0:P - turn, :])
+            if turn > 0:
+                nc.scalar.copy(out=lt[:, 0:turn, :], in_=src[:, P - turn:P, :])
 
         def pe_mm(t, j):
             if not ok(t):
@@ -291,7 +280,7 @@ def tile_dynamicconvdecoderlayer_pa_kernel(tc, h, x, ww, bw, w2, b2, gamma, beta
             cb = T[("cb", t)][:, 512 * half:512 * half + 512]
             cd = T[("cd", t, half)][:].rearrange("p t m q -> p (t m q)")
             if t < NB:
-                nc.vector.tensor_copy(out=cb, in_=cd)
+                nc.scalar.copy(out=cb, in_=cd)
             else:
                 ysb = T[("ysb", t // NB)][:, 512 * half:512 * half + 512]
                 nc.vector.scalar_tensor_tensor(out=cb, in0=ysb, scalar=msk[:, t % NB:t % NB + 1], in1=cd, op0=ALU.mult, op1=ALU.add)
@@ -415,8 +404,8 @@ def tile_dynamicconvdecoderlayer_pa_kernel(tc, h, x, ww, bw, w2, b2, gamma, beta
         for s in range(-2, NT + LAG + 4):
             a, a1, a2 = s, s - 1, s - 2
             b0, b1, b2t, b3 = s - LAG, s - LAG - 1, s - LAG - 2, s - LAG - 3
-            ct = [(ib, j) for ib in range(1, NI) for j in range(4) if s == 4 * ib + 7 + j // 1]
-            cm = [(ib, j) for ib in range(1, NI) for j in range(4) if s == 4 * ib + 8 + j // 1]
+            ct = [(ib, j) for ib in range(1, NI) for j in range(4) if s == 4 * ib + 7 + j // 2]
+            cm = [(ib, j) for ib in range(1, NI) for j in range(4) if s == 4 * ib + 8 + j // 2]
             if 0 <= s < NT - 4:
                 ld(s + 4)
             if 0 <= s < 4:
@@ -433,53 +422,48 @@ def tile_dynamicconvdecoderlayer_pa_kernel(tc, h, x, ww, bw, w2, b2, gamma, beta
                     ld_hc(ib)
             sp_reads(b0 + 2)
 
-            act_lt(b0, 0)
-            dve_qc(b2t)
-            pe_bandT(b0, 1)
-            act_lt(b0, 1)
-            pe_mm2(b2t)
-            dve_qh(a)
             dve_zb(a1)
-            pe_bandT(b0, 2)
-            act_lt(b0, 2)
-            dve_c(b1, 0)
-            dve_c(b1, 1)
-            dve_B(b3)
-            sp_store(b3)
+            dve_v(b3)
+            pe_mm(b1, 0)
+            pe_cT(b2t)
+            act_cg(b2t)
+            pe_mm(b1, 1)
+            act_lt(b0, 0)
+            act_lt(b0, 1)
+            dve_nm(b3)
+            act_sq(b3)
+            pool_rstd(b3)
+            act_hf(b0)
             pe_mm1(a)
-            pe_hT(a + 2)
-            act_hg(a + 2)
+            dve_c(b1, 0)
+            dve_qc(b2t)
+            dve_max(a1)
+            dve_sum(a2)
+            dve_A(b3)
+            dve_sub(a1)
+            act_exp(a1)
+            pe_mm(b1, 2)
             for ib, j in cm:
                 pe_cornermm(ib, j)
                 act_ysb(ib, j)
-            dve_max(a1)
-            dve_xb(b2t)
-            pe_cT(b1)
-            act_cg(b1)
-            dve_v(b2t)
-            dve_sum(a2)
-            dve_nm(b2t)
-            act_sq(b2t)
-            pool_rstd(b2t)
-            dve_sub(a1)
-            act_exp(a1)
-            pe_bandT(b0, 3)
-            act_lt(b0, 3)
-            act_hf(b0 + 1)
-            for ib, j in ct:
-                if j == 0:
-                    act_hcf(ib)
-                pe_cornerT(ib, j)
-                act_lc(ib, j)
-            dve_A(b2t)
             dve_rs(a2)
             dve_w(a2)
             sp_write(a2)
-            pe_mm(b0, 0)
-            pe_mm(b0, 1)
-            pe_mm(b0, 2)
-            pe_mm(b0, 3)
-            pe_bandT(b0 + 1, 0)
+            act_lt(b0, 2)
+            pe_hT(a + 2)
+            act_hg(a + 2)
+            dve_xb(b2t)
+            pe_mm2(b2t)
+            pe_mm(b1, 3)
+            dve_qh(a + 1)
+            dve_c(b1, 1)
+            act_lt(b0, 3)
+            for ib, j in ct:
+                if j == 0:
+                    act_hcf(ib)
+                act_lc(ib, j)
+            dve_B(b3)
+            sp_store(b3)
             if 1 <= s < 5:
                 w2_prep(2 * (s - 1))
                 w2_prep(2 * (s - 1) + 1)

@@ -160,34 +160,24 @@ def tile_dynamicconvdecoderlayer_pa_kernel(tc, h, x, ww, bw, w2, b2, gamma, beta
             if not ok(t):
                 return
             zb = p2.tile([P, H, K], F32, name="zb", tag="zb")
-            nc.vector.tensor_tensor(out=zb[:].rearrange("p n k -> p (n k)"), in0=T[("z", t)][:], in1=bw_bc[:], op=ALU.add)
+            nc.vector.scalar_tensor_tensor(out=zb[:].rearrange("p n k -> p (n k)"), in0=T[("z", t)][:], scalar=-1.0, in1=bw_bc[:], op0=ALU.mult, op1=ALU.subtract)
             T[("zb", t)] = zb
 
         def dve_max(t):
             if not ok(t):
                 return
             mx = p2.tile([P, H], F32, name="mx", tag="mx")
-            nc.vector.tensor_reduce(out=mx[:], in_=T[("zb", t)][:], axis=AX.X, op=ALU.max)
+            nc.vector.tensor_reduce(out=mx[:], in_=T[("zb", t)][:], axis=AX.X, op=ALU.min)
             T[("mx", t)] = mx
-
-        def dve_sub(t):
-            if not ok(t):
-                return
-            zb = T[("zb", t)]
-            nc.vector.tensor_tensor(out=zb[:], in0=zb[:], in1=T[("mx", t)][:].unsqueeze(2).to_broadcast([P, H, K]), op=ALU.subtract)
 
         def act_exp(t):
             if not ok(t):
                 return
             ex = p2.tile([P, H, K], F32, name="ex", tag="ex")
-            nc.scalar.activation(out=ex[:], in_=T[("zb", t)][:], func=ACT.Exp)
-            T[("ex", t)] = ex
-
-        def dve_sum(t):
-            if not ok(t):
-                return
             sums = p2.tile([P, H], F32, name="sums", tag="sums")
-            nc.vector.tensor_reduce(out=sums[:], in_=T[("ex", t)][:], axis=AX.X, op=ALU.add)
+            for n in range(H):
+                nc.scalar.activation(out=ex[:, n, :], in_=T[("zb", t)][:, n, :], func=ACT.Exp, bias=T[("mx", t)][:, n:n + 1], scale=-1.0, accum_out=sums[:, n:n + 1])
+            T[("ex", t)] = ex
             T[("sums", t)] = sums
 
         def dve_rs(t):
@@ -234,19 +224,18 @@ def tile_dynamicconvdecoderlayer_pa_kernel(tc, h, x, ww, bw, w2, b2, gamma, beta
             T[("hcf", ib)] = hcf
 
         def pe_cornermm(ib, j):
-            yk = ps_t.tile([P, 4, 4, 16], F32, name="yk", tag="tp")
+            yk = ps_t.tile([P, 256], F32, name="yk", tag="tp")
             lc = T[("lc", ib, j)]
             hcf = T[("hcf", ib)]
             for q in range(4):
                 n = 4 * j + q
-                nc.tensor.matmul(out=yk[:, :, q, :], lhsT=lc[:, q, :], rhs=hcf[:, R * n:R * n + R], start=True, stop=True)
+                nc.tensor.matmul(out=yk[:, R * q:R * q + R], lhsT=lc[:, q, :], rhs=hcf[:, R * n:R * n + R], start=True, stop=True)
             T[("yk", ib, j)] = yk
 
         def act_ysb(ib, j):
             if j == 0:
                 T[("ysb", ib)] = p2.tile([P, C], F32, name="ysb", tag="ysb")
-            ysb = T[("ysb", ib)][:, 512 * (j // 2):512 * (j // 2) + 512].rearrange("p (t m q) -> p t (m q)", t=4, m=8)
-            nc.scalar.copy(out=ysb[:, :, 64 * (j % 2):64 * (j % 2) + 64], in_=T[("yk", ib, j)][:].rearrange("p t m q -> p t (m q)"))
+            nc.scalar.copy(out=T[("ysb", ib)][:, 256 * j:256 * j + 256], in_=T[("yk", ib, j)][:])
 
         def act_lt(t, j):
             if not ok(t):
@@ -264,26 +253,27 @@ def tile_dynamicconvdecoderlayer_pa_kernel(tc, h, x, ww, bw, w2, b2, gamma, beta
             if not ok(t):
                 return
             if j % 2 == 0:
-                T[("cd", t, j // 2)] = ps_c.tile([P, 4, 8, 16], F32, name="cd", tag="cd")
+                T[("cd", t, j // 2)] = ps_c.tile([P, 512], F32, name="cd", tag="cd")
             cd = T[("cd", t, j // 2)]
             lt = T[("lt", t)]
             hf = T[("hf", t)]
             for q in range(4):
                 n = 4 * j + q
-                nc.tensor.matmul(out=cd[:, :, n % 8, :], lhsT=lt[:, n, :], rhs=hf[:, R * n:R * n + R], start=True, stop=True)
+                nc.tensor.matmul(out=cd[:, R * (n % 8):R * (n % 8) + R], lhsT=lt[:, n, :], rhs=hf[:, R * n:R * n + R], start=True, stop=True)
 
         def dve_c(t, half):
             if not ok(t):
                 return
             if half == 0:
                 T[("cb", t)] = p2.tile([P, C], BF16, name="cb", tag="cb")
-            cb = T[("cb", t)][:, 512 * half:512 * half + 512]
-            cd = T[("cd", t, half)][:].rearrange("p t m q -> p (t m q)")
+            cb = T[("cb", t)][:, 512 * half:512 * half + 512].rearrange("p (t m q) -> p m t q", t=4, m=8)
+            cd = T[("cd", t, half)][:].rearrange("p (m t q) -> p m t q", t=4, m=8)
             if t < NB:
                 nc.scalar.copy(out=cb, in_=cd)
             else:
-                ysb = T[("ysb", t // NB)][:, 512 * half:512 * half + 512]
-                nc.vector.scalar_tensor_tensor(out=cb, in0=ysb, scalar=msk[:, t % NB:t % NB + 1], in1=cd, op0=ALU.mult, op1=ALU.add)
+                ysb = T[("ysb", t // NB)][:, 512 * half:512 * half + 512].rearrange("p (m t q) -> p m t q", t=4, m=8)
+                for u in range(4):
+                    nc.vector.scalar_tensor_tensor(out=cb[:, :, u, :], in0=ysb[:, :, u, :], scalar=msk[:, t % NB:t % NB + 1], in1=cd[:, :, u, :], op0=ALU.mult, op1=ALU.add)
 
         def pe_cT(t):
             if not ok(t):
@@ -435,14 +425,16 @@ def tile_dynamicconvdecoderlayer_pa_kernel(tc, h, x, ww, bw, w2, b2, gamma, beta
             pool_rstd(b3)
             act_hf(b0)
             pe_mm1(a)
+            dve_max(a1)
             dve_c(b1, 0)
             dve_qc(b2t)
-            dve_max(a1)
-            dve_sum(a2)
-            dve_A(b3)
-            dve_sub(a1)
             act_exp(a1)
+            dve_A(b3)
             pe_mm(b1, 2)
+            for ib, j in ct:
+                if j == 0:
+                    act_hcf(ib)
+                act_lc(ib, j)
             for ib, j in cm:
                 pe_cornermm(ib, j)
                 act_ysb(ib, j)
@@ -458,10 +450,6 @@ def tile_dynamicconvdecoderlayer_pa_kernel(tc, h, x, ww, bw, w2, b2, gamma, beta
             dve_qh(a + 1)
             dve_c(b1, 1)
             act_lt(b0, 3)
-            for ib, j in ct:
-                if j == 0:
-                    act_hcf(ib)
-                act_lc(ib, j)
             dve_B(b3)
             sp_store(b3)
             if 1 <= s < 5:

@@ -245,9 +245,10 @@ def tile_dynamicconvdecoderlayer_pa_kernel(tc, h, x, ww, bw, w2, b2, gamma, beta
             lt = T[("lt", t)][:, 4 * j:4 * j + 4, :].rearrange("p n i -> p i n")
             src = bands[t // 2 % 2][:, :, H * (t % 2) + 4 * j:H * (t % 2) + 4 * j + 4]
             turn = 32 * (t % NB)
-            nc.scalar.copy(out=lt[:, turn:P, :], in_=src[:, 0:P - turn, :])
+            copy = nc.scalar.copy if j < 2 else nc.vector.tensor_copy
+            copy(out=lt[:, turn:P, :], in_=src[:, 0:P - turn, :])
             if turn > 0:
-                nc.scalar.copy(out=lt[:, 0:turn, :], in_=src[:, P - turn:P, :])
+                copy(out=lt[:, 0:turn, :], in_=src[:, P - turn:P, :])
 
         def pe_mm(t, j):
             if not ok(t):
@@ -414,39 +415,39 @@ def tile_dynamicconvdecoderlayer_pa_kernel(tc, h, x, ww, bw, w2, b2, gamma, beta
 
             dve_zb(a1)
             dve_v(b3)
+            act_hf(b0)
             pe_mm(b1, 0)
-            pe_cT(b2t)
-            act_cg(b2t)
-            pe_mm(b1, 1)
             act_lt(b0, 0)
             act_lt(b0, 1)
             dve_nm(b3)
+            pe_cT(b2t)
+            act_cg(b2t)
+            pe_mm(b1, 1)
             act_sq(b3)
             pool_rstd(b3)
-            act_hf(b0)
             pe_mm1(a)
             dve_max(a1)
             dve_c(b1, 0)
-            dve_qc(b2t)
             act_exp(a1)
+            dve_qc(b2t)
             dve_A(b3)
             pe_mm(b1, 2)
-            for ib, j in ct:
-                if j == 0:
-                    act_hcf(ib)
-                act_lc(ib, j)
             for ib, j in cm:
                 pe_cornermm(ib, j)
                 act_ysb(ib, j)
+            pe_hT(a + 2)
+            act_hg(a + 2)
             dve_rs(a2)
             dve_w(a2)
             sp_write(a2)
             act_lt(b0, 2)
-            pe_hT(a + 2)
-            act_hg(a + 2)
             dve_xb(b2t)
             pe_mm2(b2t)
             pe_mm(b1, 3)
+            for ib, j in ct:
+                if j == 0:
+                    act_hcf(ib)
+                act_lc(ib, j)
             dve_qh(a + 1)
             dve_c(b1, 1)
             act_lt(b0, 3)

@@ -1,4 +1,5 @@
 from contextlib import ExitStack
+from functools import partial
 
 import concourse.mybir as mybir
 from concourse.masks import make_identity
@@ -116,12 +117,10 @@ def tile_dynamicconvdecoderlayer_pa_kernel(tc, h, x, ww, bw, w2, b2, gamma, beta
 
         def pe_hT(t):
             if not ok(t):
-                return
+                return []
             tp = ps_t.tile([P, 4, P], F32, name="tp", tag="tp")
-            for gu in range(4):
-                g, u = divmod(gu, 2)
-                nc.tensor.transpose(tp[:, gu, :], hbs[t][:].bitcast(F32)[:, 256 * g + u:256 * g + 256:2], idf[:])
             T[("hT", t)] = tp
+            return [partial(nc.tensor.transpose, tp[:, 2 * g + u, :], hbs[t][:].bitcast(F32)[:, 256 * g + u:256 * g + 256:2], idf[:]) for g in range(2) for u in range(2)]
 
         def act_hg(t):
             if not ok(t):
@@ -148,13 +147,12 @@ def tile_dynamicconvdecoderlayer_pa_kernel(tc, h, x, ww, bw, w2, b2, gamma, beta
 
         def pe_mm1(t):
             if not ok(t):
-                return
+                return []
             hq, hs = T[("hq", t)]
             z = ps_z.tile([P, 512], F32, name="z", tag="z")
-            for g in range(2):
-                nc.tensor.matmul_mx(out=z[:], lhsT=hq[:, P * g:P * g + P].bitcast(FP8X4), lhsT_scale=hs[:, P * g:P * g + P],
-                                    rhs=wwq[:, g, :].bitcast(FP8X4), rhs_scale=wws[:, g, :], start=(g == 0), stop=(g == 1))
             T[("z", t)] = z
+            return [partial(nc.tensor.matmul_mx, out=z[:], lhsT=hq[:, P * g:P * g + P].bitcast(FP8X4), lhsT_scale=hs[:, P * g:P * g + P],
+                            rhs=wwq[:, g, :].bitcast(FP8X4), rhs_scale=wws[:, g, :], start=(g == 0), stop=(g == 1)) for g in range(2)]
 
         def dve_zb(t):
             if not ok(t):
@@ -213,29 +211,27 @@ def tile_dynamicconvdecoderlayer_pa_kernel(tc, h, x, ww, bw, w2, b2, gamma, beta
             src = flat[base:base + 32 * 2016].rearrange("(i w) -> i w", w=2016)[:, 0:1024].rearrange("i (s c) -> s i c", c=2 * H)
             nc.sync.dma_start(out=corner[32 * b:32 * b + 32, 32 * b:32 * b + 32, :], in_=src[:, :, H * (b % 2):H * (b % 2) + H])
 
-        def act_lc(ib, j):
-            lc = p2.tile([P, 4, P], F32, name="lc", tag="lc", bufs=4)
-            nc.scalar.copy(out=lc[:].rearrange("p n i -> p i n"), in_=corner[:, :, 4 * j:4 * j + 4])
-            T[("lc", ib, j)] = lc
+        def act_lc(ib, half):
+            lc = p2.tile([P, 8, P], F32, name="lc", tag="lc")
+            for j in range(2):
+                nc.scalar.copy(out=lc[:, 4 * j:4 * j + 4, :].rearrange("p n i -> p i n"), in_=corner[:, :, 8 * half + 4 * j:8 * half + 4 * j + 4])
+            T[("lc", ib, half)] = lc
 
         def act_hcf(ib):
             hcf = p2.tile([P, C], F32, name="hcf", tag="hcf")
             nc.scalar.copy(out=hcf[:].rearrange("p (n t q) -> p n t q", t=4, q=16), in_=T[("hcb", ib)][:].rearrange("p (n q t) -> p n t q", t=4, q=16))
             T[("hcf", ib)] = hcf
 
-        def pe_cornermm(ib, j):
-            yk = ps_t.tile([P, 256], F32, name="yk", tag="tp")
-            lc = T[("lc", ib, j)]
-            hcf = T[("hcf", ib)]
-            for q in range(4):
-                n = 4 * j + q
-                nc.tensor.matmul(out=yk[:, R * q:R * q + R], lhsT=lc[:, q, :], rhs=hcf[:, R * n:R * n + R], start=True, stop=True)
-            T[("yk", ib, j)] = yk
+        def pe_cornermm(ib, half):
+            yk = ps_t.tile([P, 512], F32, name="yk", tag="tp")
+            T[("yk", ib, half)] = yk
+            return [partial(nc.tensor.matmul, out=yk[:, R * m:R * m + R], lhsT=T[("lc", ib, half)][:, m, :], rhs=T[("hcf", ib)][:, R * (8 * half + m):R * (8 * half + m) + R],
+                            start=True, stop=True) for m in range(8)]
 
-        def act_ysb(ib, j):
-            if j == 0:
+        def act_ysb(ib, half):
+            if half == 0:
                 T[("ysb", ib)] = p2.tile([P, C], F32, name="ysb", tag="ysb")
-            nc.scalar.copy(out=T[("ysb", ib)][:, 256 * j:256 * j + 256], in_=T[("yk", ib, j)][:])
+            nc.scalar.copy(out=T[("ysb", ib)][:, 512 * half:512 * half + 512], in_=T[("yk", ib, half)][:])
 
         def act_lt(t, j):
             if not ok(t):
@@ -250,17 +246,13 @@ def tile_dynamicconvdecoderlayer_pa_kernel(tc, h, x, ww, bw, w2, b2, gamma, beta
             if turn > 0:
                 copy(out=lt[:, 0:turn, :], in_=src[:, P - turn:P, :])
 
-        def pe_mm(t, j):
+        def pe_mm(t, half):
             if not ok(t):
-                return
-            if j % 2 == 0:
-                T[("cd", t, j // 2)] = ps_c.tile([P, 512], F32, name="cd", tag="cd")
-            cd = T[("cd", t, j // 2)]
-            lt = T[("lt", t)]
-            hf = T[("hf", t)]
-            for q in range(4):
-                n = 4 * j + q
-                nc.tensor.matmul(out=cd[:, R * (n % 8):R * (n % 8) + R], lhsT=lt[:, n, :], rhs=hf[:, R * n:R * n + R], start=True, stop=True)
+                return []
+            cd = ps_c.tile([P, 512], F32, name="cd", tag="cd")
+            T[("cd", t, half)] = cd
+            return [partial(nc.tensor.matmul, out=cd[:, R * m:R * m + R], lhsT=T[("lt", t)][:, 8 * half + m, :], rhs=T[("hf", t)][:, R * (8 * half + m):R * (8 * half + m) + R],
+                            start=True, stop=True) for m in range(8)]
 
         def dve_c(t, half):
             if not ok(t):
@@ -278,13 +270,10 @@ def tile_dynamicconvdecoderlayer_pa_kernel(tc, h, x, ww, bw, w2, b2, gamma, beta
 
         def pe_cT(t):
             if not ok(t):
-                return
+                return []
             tpb = ps_t.tile([P, 8, P], BF16, name="tpb", tag="tp")
-            cb = T[("cb", t)]
-            off = 32 * (t % NB)
-            for ch in range(8):
-                nc.tensor.transpose(tpb[:, ch, :], cb[:, P * ch:P * ch + P], idb[:, off:off + P])
             T[("cT", t)] = tpb
+            return [partial(nc.tensor.transpose, tpb[:, ch, :], T[("cb", t)][:, P * ch:P * ch + P], idb[:, 32 * (t % NB):32 * (t % NB) + P]) for ch in range(8)]
 
         def act_cg(t):
             if not ok(t):
@@ -303,15 +292,24 @@ def tile_dynamicconvdecoderlayer_pa_kernel(tc, h, x, ww, bw, w2, b2, gamma, beta
 
         def pe_mm2(t):
             if not ok(t):
-                return
+                return []
             cq, cs = T[("cq", t)]
+            passes = []
             for e2 in range(2):
                 yp = ps_y.tile([P, 512], F32, name="yp", tag="yp")
-                for g in range(2):
-                    nc.tensor.matmul_mx(out=yp[:], lhsT=cq[:, P * g:P * g + P].bitcast(FP8X4), lhsT_scale=cs[:, P * g:P * g + P],
-                                        rhs=w2q[:, g, 512 * e2:512 * e2 + 512].bitcast(FP8X4), rhs_scale=w2s[:, g, 512 * e2:512 * e2 + 512],
-                                        start=(g == 0), stop=(g == 1))
                 T[("yp", t, e2)] = yp
+                for g in range(2):
+                    passes.append(partial(nc.tensor.matmul_mx, out=yp[:], lhsT=cq[:, P * g:P * g + P].bitcast(FP8X4), lhsT_scale=cs[:, P * g:P * g + P],
+                                          rhs=w2q[:, g, 512 * e2:512 * e2 + 512].bitcast(FP8X4), rhs_scale=w2s[:, g, 512 * e2:512 * e2 + 512],
+                                          start=(g == 0), stop=(g == 1)))
+            return passes
+
+        def weave(narrow, others):
+            n = max(len(narrow), len(others))
+            for i in range(n):
+                for group in (narrow, others):
+                    for k in range(i * len(group) // n, (i + 1) * len(group) // n):
+                        group[k]()
 
         def dve_xb(t):
             if not ok(t):
@@ -395,8 +393,8 @@ def tile_dynamicconvdecoderlayer_pa_kernel(tc, h, x, ww, bw, w2, b2, gamma, beta
         for s in range(-2, NT + LAG + 4):
             a, a1, a2 = s, s - 1, s - 2
             b0, b1, b2t, b3 = s - LAG, s - LAG - 1, s - LAG - 2, s - LAG - 3
-            ct = [(ib, j) for ib in range(1, NI) for j in range(4) if s == 4 * ib + 7 + j // 2]
-            cm = [(ib, j) for ib in range(1, NI) for j in range(4) if s == 4 * ib + 8 + j // 2]
+            ct = [(ib, half) for ib in range(1, NI) for half in range(2) if s == 4 * ib + 7 + half]
+            cm = [(ib, half) for ib in range(1, NI) for half in range(2) if s == 4 * ib + 8 + half]
             if 0 <= s < NT - 4:
                 ld(s + 4)
             if 0 <= s < 4:
@@ -416,38 +414,39 @@ def tile_dynamicconvdecoderlayer_pa_kernel(tc, h, x, ww, bw, w2, b2, gamma, beta
             dve_zb(a1)
             dve_v(b3)
             act_hf(b0)
-            pe_mm(b1, 0)
+            cT = pe_cT(b2t)
+            mm = pe_mm(b1, 0)
+            weave(mm, cT)
             act_lt(b0, 0)
             act_lt(b0, 1)
             dve_nm(b3)
-            pe_cT(b2t)
             act_cg(b2t)
-            pe_mm(b1, 1)
             act_sq(b3)
             pool_rstd(b3)
-            pe_mm1(a)
             dve_max(a1)
             dve_c(b1, 0)
             act_exp(a1)
             dve_qc(b2t)
             dve_A(b3)
-            pe_mm(b1, 2)
-            for ib, j in cm:
-                pe_cornermm(ib, j)
-                act_ysb(ib, j)
-            pe_hT(a + 2)
+            hT = pe_hT(a + 2)
+            cmm = []
+            for ib, half in cm:
+                cmm = cmm + pe_cornermm(ib, half)
+            mm = pe_mm(b1, 1)
+            weave(mm[0:4] + cmm, pe_mm1(a) + hT)
             act_hg(a + 2)
+            for ib, half in cm:
+                act_ysb(ib, half)
             dve_rs(a2)
             dve_w(a2)
             sp_write(a2)
             act_lt(b0, 2)
             dve_xb(b2t)
-            pe_mm2(b2t)
-            pe_mm(b1, 3)
-            for ib, j in ct:
-                if j == 0:
+            weave(mm[4:8], pe_mm2(b2t))
+            for ib, half in ct:
+                if half == 0:
                     act_hcf(ib)
-                act_lc(ib, j)
+                act_lc(ib, half)
             dve_qh(a + 1)
             dve_c(b1, 1)
             act_lt(b0, 3)

@@ -24,7 +24,7 @@ K = 32
 R = 64
 SL = 64
 EPS = 1e-5
-LAG = 8
+LAG = 7
 
 
 def tile_dynamicconvdecoderlayer_pa_kernel(tc, h, x, ww, bw, w2, b2, gamma, beta, out):
@@ -79,13 +79,11 @@ def tile_dynamicconvdecoderlayer_pa_kernel(tc, h, x, ww, bw, w2, b2, gamma, beta
         for t in range(1, 4):
             ld(t)
 
-        idf = const.tile([P, P], F32, name="idf")
-        make_identity(nc, idf[:])
-        idb = const.tile([P, 2 * P], BF16, name="idb")
-        nc.vector.tensor_copy(out=idb[:, 0:P], in_=idf[:])
-        nc.vector.tensor_copy(out=idb[:, P:2 * P], in_=idf[:])
+        idf = const.tile([P, 2 * P], F32, name="idf")
+        make_identity(nc, idf[:, 0:P])
+        nc.vector.tensor_copy(out=idf[:, P:2 * P], in_=idf[:, 0:P])
         msk = const.tile([P, 4], F32, name="msk")
-        nc.vector.tensor_reduce(out=msk[:], in_=idf[:].rearrange("p (j c) -> p j c", c=32), axis=AX.X, op=ALU.add)
+        nc.vector.tensor_reduce(out=msk[:], in_=idf[:, 0:P].rearrange("p (j c) -> p j c", c=32), axis=AX.X, op=ALU.add)
         nhalf = const.tile([P, 1], F32, name="nhalf")
         nc.gpsimd.memset(nhalf[:], -0.5)
         wwq = const.tile([P, 2, 512], U32, name="wwq", align_bytes=64)
@@ -107,7 +105,7 @@ def tile_dynamicconvdecoderlayer_pa_kernel(tc, h, x, ww, bw, w2, b2, gamma, beta
             tp = ps_t.tile([P, 4, P], F32, name="tp", tag="tp")
             for gu in range(4):
                 g, u = divmod(gu, 2)
-                nc.tensor.transpose(tp[:, gu, :], raws[rt][:].bitcast(F32)[:, 256 * g + u:256 * g + 256:2], idf[:])
+                nc.tensor.transpose(tp[:, gu, :], raws[rt][:].bitcast(F32)[:, 256 * g + u:256 * g + 256:2], idf[:, 0:P])
             if rt % 2 == 0:
                 nc.vector.tensor_copy(out=gww32[:, :, P * rt:P * rt + P, :], in_=tp[:].rearrange("p (g u) r -> p g r u", g=2))
             else:
@@ -120,12 +118,12 @@ def tile_dynamicconvdecoderlayer_pa_kernel(tc, h, x, ww, bw, w2, b2, gamma, beta
                 return []
             tp = ps_t.tile([P, 4, P], F32, name="tp", tag="tp")
             T[("hT", t)] = tp
-            return [partial(nc.tensor.transpose, tp[:, 2 * g + u, :], hbs[t][:].bitcast(F32)[:, 256 * g + u:256 * g + 256:2], idf[:]) for g in range(2) for u in range(2)]
+            return [partial(nc.tensor.transpose, tp[:, 2 * g + u, :], hbs[t][:].bitcast(F32)[:, 256 * g + u:256 * g + 256:2], idf[:, 0:P]) for g in range(2) for u in range(2)]
 
         def act_hg(t):
             if not ok(t):
                 return
-            hg = p2.tile([P, C], BF16, name="hg", tag="hg", align_bytes=64)
+            hg = p3.tile([P, C], BF16, name="hg", tag="hg", align_bytes=64)
             nc.scalar.copy(out=hg[:].bitcast(F32).rearrange("p (g r u) -> p g r u", g=2, u=2),
                            in_=T[("hT", t)][:].rearrange("p (g u) r -> p g r u", g=2))
             T[("hg", t)] = hg
@@ -134,7 +132,7 @@ def tile_dynamicconvdecoderlayer_pa_kernel(tc, h, x, ww, bw, w2, b2, gamma, beta
             if not ok(t):
                 return
             hf = p2.tile([P, C], F32, name="hf", tag="hf")
-            nc.scalar.copy(out=hf[:].rearrange("p (n t q) -> p n t q", t=4, q=16), in_=hbs[t][:].rearrange("p (n q t) -> p n t q", t=4, q=16))
+            nc.scalar.copy(out=hf[:], in_=hbs[t][:])
             T[("hf", t)] = hf
 
         def dve_qh(t):
@@ -219,7 +217,7 @@ def tile_dynamicconvdecoderlayer_pa_kernel(tc, h, x, ww, bw, w2, b2, gamma, beta
 
         def act_hcf(ib):
             hcf = p2.tile([P, C], F32, name="hcf", tag="hcf")
-            nc.scalar.copy(out=hcf[:].rearrange("p (n t q) -> p n t q", t=4, q=16), in_=T[("hcb", ib)][:].rearrange("p (n q t) -> p n t q", t=4, q=16))
+            nc.scalar.copy(out=hcf[:], in_=T[("hcb", ib)][:])
             T[("hcf", ib)] = hcf
 
         def pe_cornermm(ib, half):
@@ -259,27 +257,29 @@ def tile_dynamicconvdecoderlayer_pa_kernel(tc, h, x, ww, bw, w2, b2, gamma, beta
                 return
             if half == 0:
                 T[("cb", t)] = p2.tile([P, C], BF16, name="cb", tag="cb")
-            cb = T[("cb", t)][:, 512 * half:512 * half + 512].rearrange("p (t m q) -> p m t q", t=4, m=8)
-            cd = T[("cd", t, half)][:].rearrange("p (m t q) -> p m t q", t=4, m=8)
+            cb = T[("cb", t)][:, 512 * half:512 * half + 512].rearrange("p (u k e) -> p u k e", u=2, e=2)
+            cd = T[("cd", t, half)][:].rearrange("p (k u e) -> p u k e", u=2, e=2)
             if t < NB:
                 nc.scalar.copy(out=cb, in_=cd)
             else:
-                ysb = T[("ysb", t // NB)][:, 512 * half:512 * half + 512].rearrange("p (m t q) -> p m t q", t=4, m=8)
-                for u in range(4):
-                    nc.vector.scalar_tensor_tensor(out=cb[:, :, u, :], in0=ysb[:, :, u, :], scalar=msk[:, t % NB:t % NB + 1], in1=cd[:, :, u, :], op0=ALU.mult, op1=ALU.add)
+                ysb = T[("ysb", t // NB)][:, 512 * half:512 * half + 512].rearrange("p (k u e) -> p u k e", u=2, e=2)
+                for u in range(2):
+                    nc.vector.scalar_tensor_tensor(out=cb[:, u, :, :], in0=ysb[:, u, :, :], scalar=msk[:, t % NB:t % NB + 1], in1=cd[:, u, :, :], op0=ALU.mult, op1=ALU.add)
 
         def pe_cT(t):
             if not ok(t):
                 return []
-            tpb = ps_t.tile([P, 8, P], BF16, name="tpb", tag="tp")
-            T[("cT", t)] = tpb
-            return [partial(nc.tensor.transpose, tpb[:, ch, :], T[("cb", t)][:, P * ch:P * ch + P], idb[:, 32 * (t % NB):32 * (t % NB) + P]) for ch in range(8)]
+            tp = ps_t.tile([P, 4, P], F32, name="tp", tag="tp")
+            T[("cT", t)] = tp
+            turn = 32 * (t % NB)
+            return [partial(nc.tensor.transpose, tp[:, gu, :], T[("cb", t)][:].bitcast(F32)[:, P * gu:P * gu + P], idf[:, turn:turn + P]) for gu in range(4)]
 
         def act_cg(t):
             if not ok(t):
                 return
             cg = p2.tile([P, C], BF16, name="cg", tag="cg", align_bytes=64)
-            nc.scalar.copy(out=cg[:].rearrange("p (g r t) -> p g r t", g=2, t=4), in_=T[("cT", t)][:].rearrange("p (g t) r -> p g r t", g=2))
+            nc.scalar.copy(out=cg[:].bitcast(F32).rearrange("p (g r u) -> p g r u", g=2, u=2),
+                           in_=T[("cT", t)][:].rearrange("p (g u) r -> p g r u", g=2))
             T[("cg", t)] = cg
 
         def dve_qc(t):
@@ -381,25 +381,26 @@ def tile_dynamicconvdecoderlayer_pa_kernel(tc, h, x, ww, bw, w2, b2, gamma, beta
         def w2_prep(rt):
             if rt == 0:
                 T["gw2"] = [p2.tile([P, 4096], BF16, name="gw2", tag="lt", align_bytes=64) for g in range(2)]
-            raw = T[("raw", rt)]
-            tpb = ps_t.tile([P, 8, P], BF16, name="tpb", tag="tp")
-            for gt in range(8):
-                g, t = divmod(gt, 4)
-                nc.tensor.transpose(tpb[:, gt, :], raw[:, 512 * g + t:512 * g + 512:4], idb[:, 0:P])
+            tp = ps_t.tile([P, 4, P], F32, name="tp", tag="tp")
+            for gu in range(4):
+                g, u = divmod(gu, 2)
+                nc.tensor.transpose(tp[:, gu, :], T[("raw", rt)][:].bitcast(F32)[:, 256 * g + u:256 * g + 256:2], idf[:, 0:P])
             for g in range(2):
-                nc.scalar.copy(out=T["gw2"][g][:].rearrange("p (c t) -> p c t", t=4)[:, P * rt:P * rt + P, :],
-                               in_=tpb[:, 4 * g:4 * g + 4, :].rearrange("p t r -> p r t"))
+                nc.scalar.copy(out=T["gw2"][g][:].bitcast(F32).rearrange("p (c u) -> p c u", u=2)[:, P * rt:P * rt + P, :],
+                               in_=tp[:, 2 * g:2 * g + 2, :].rearrange("p u r -> p r u"))
 
-        for s in range(-2, NT + LAG + 4):
+        for s in range(-3, NT + LAG + 4):
             a, a1, a2 = s, s - 1, s - 2
             b0, b1, b2t, b3 = s - LAG, s - LAG - 1, s - LAG - 2, s - LAG - 3
-            ct = [(ib, half) for ib in range(1, NI) for half in range(2) if s == 4 * ib + 7 + half]
-            cm = [(ib, half) for ib in range(1, NI) for half in range(2) if s == 4 * ib + 8 + half]
-            if 0 <= s < NT - 4:
-                ld(s + 4)
-            if 0 <= s < 4:
-                w2_load(2 * s)
-                w2_load(2 * s + 1)
+            ct = [(ib, half) for ib in range(1, NI) for half in range(2) if s == 4 * ib + 6 + half]
+            cm = [(ib, half) for ib in range(1, NI) for half in range(2) if s == 4 * ib + 7 + half]
+            if 0 <= s < 3:
+                for t in range(4 * s + 4, 4 * s + 8):
+                    ld(t)
+            if s in (0, 1, 3, 4):
+                rt = 2 * s if s < 2 else 2 * s - 2
+                w2_load(rt)
+                w2_load(rt + 1)
             if s == 2:
                 nc.sync.dma_start(out=b2_bc[:], in_=b2.partition_broadcast(P))
             if s == 3:
@@ -407,9 +408,11 @@ def tile_dynamicconvdecoderlayer_pa_kernel(tc, h, x, ww, bw, w2, b2, gamma, beta
                 nc.sync.dma_start(out=be_bc[:], in_=beta.partition_broadcast(P))
             ld_x(b0)
             for ib in range(1, NI):
-                if s == 4 * ib + 5:
+                if s == 4 * ib + 4:
                     ld_hc(ib)
-            sp_reads(b0 + 2)
+            for t in range(0, NT, 2):
+                if s == t + (4 if t < 4 else LAG - 2):
+                    sp_reads(t)
 
             dve_zb(a1)
             dve_v(b3)
@@ -428,13 +431,13 @@ def tile_dynamicconvdecoderlayer_pa_kernel(tc, h, x, ww, bw, w2, b2, gamma, beta
             act_exp(a1)
             dve_qc(b2t)
             dve_A(b3)
-            hT = pe_hT(a + 2)
+            hT = pe_hT(a + 3)
             cmm = []
             for ib, half in cm:
                 cmm = cmm + pe_cornermm(ib, half)
             mm = pe_mm(b1, 1)
             weave(mm[0:4] + cmm, pe_mm1(a) + hT)
-            act_hg(a + 2)
+            act_hg(a + 3)
             for ib, half in cm:
                 act_ysb(ib, half)
             dve_rs(a2)
@@ -452,13 +455,13 @@ def tile_dynamicconvdecoderlayer_pa_kernel(tc, h, x, ww, bw, w2, b2, gamma, beta
             act_lt(b0, 3)
             dve_B(b3)
             sp_store(b3)
-            if 1 <= s < 5:
-                w2_prep(2 * (s - 1))
-                w2_prep(2 * (s - 1) + 1)
-            if s == 5:
+            if 2 <= s < 6:
+                w2_prep(2 * (s - 2))
+                w2_prep(2 * (s - 2) + 1)
+            if s == 6:
                 for g in range(2):
                     nc.vector.quantize_mx(out=w2q[:, g, :].bitcast(FP8X4), scales=w2s[:, g, :], in_=T["gw2"][g][:])
             for ib in range(1, NI):
-                if s == 4 * ib + 6:
+                if s == 4 * ib + 5:
                     for b in range(NB):
                         sp_corner(ib, b)

@@ -34,6 +34,7 @@ def tile_dynamicconvdecoderlayer_pa_kernel(tc, h, x, ww, bw, w2, b2, gamma, beta
         wst = ctx.enter_context(tc.tile_pool(name="wst", bufs=4))
         p2 = ctx.enter_context(tc.tile_pool(name="p2", bufs=2))
         p3 = ctx.enter_context(tc.tile_pool(name="p3", bufs=3))
+        hgp = ctx.enter_context(tc.tile_pool(name="hgp", bufs=7))
         p1 = ctx.enter_context(tc.tile_pool(name="p1", bufs=1))
         ps_t = ctx.enter_context(tc.psum_pool(name="ps_t", bufs=3))
         ps_z = ctx.enter_context(tc.psum_pool(name="ps_z", bufs=1))
@@ -123,7 +124,7 @@ def tile_dynamicconvdecoderlayer_pa_kernel(tc, h, x, ww, bw, w2, b2, gamma, beta
         def act_hg(t):
             if not ok(t):
                 return
-            hg = p3.tile([P, C], BF16, name="hg", tag="hg", align_bytes=64)
+            hg = hgp.tile([P, C], BF16, name="hg", tag="hg", align_bytes=64)
             nc.scalar.copy(out=hg[:].bitcast(F32).rearrange("p (g r u) -> p g r u", g=2, u=2),
                            in_=T[("hT", t)][:].rearrange("p (g u) r -> p g r u", g=2))
             T[("hg", t)] = hg
@@ -389,9 +390,12 @@ def tile_dynamicconvdecoderlayer_pa_kernel(tc, h, x, ww, bw, w2, b2, gamma, beta
                 nc.scalar.copy(out=T["gw2"][g][:].bitcast(F32).rearrange("p (c u) -> p c u", u=2)[:, P * rt:P * rt + P, :],
                                in_=tp[:, 2 * g:2 * g + 2, :].rearrange("p u r -> p r u"))
 
-        for s in range(-3, NT + LAG + 4):
+        def ahead(s):
+            return s + 4 + min(max(s, 0), 3)
+
+        for s in range(-3, NT + LAG + 5):
             a, a1, a2 = s, s - 1, s - 2
-            b0, b1, b2t, b3 = s - LAG, s - LAG - 1, s - LAG - 2, s - LAG - 3
+            b0, b1, b2t, b3, b4 = s - LAG, s - LAG - 1, s - LAG - 2, s - LAG - 3, s - LAG - 4
             ct = [(ib, half) for ib in range(1, NI) for half in range(2) if s == 4 * ib + 6 + half]
             cm = [(ib, half) for ib in range(1, NI) for half in range(2) if s == 4 * ib + 7 + half]
             if 0 <= s < 3:
@@ -419,27 +423,33 @@ def tile_dynamicconvdecoderlayer_pa_kernel(tc, h, x, ww, bw, w2, b2, gamma, beta
             act_hf(b0)
             cT = pe_cT(b2t)
             mm = pe_mm(b1, 0)
-            weave(mm, cT)
+            weave(mm[0:3], [])
+            weave(mm[3:8], cT)
             act_lt(b0, 0)
             act_lt(b0, 1)
             dve_nm(b3)
             act_cg(b2t)
             act_sq(b3)
             pool_rstd(b3)
+            dve_B(b4)
+            sp_store(b4)
             dve_max(a1)
-            dve_c(b1, 0)
             act_exp(a1)
             dve_qc(b2t)
-            dve_A(b3)
-            hT = pe_hT(a + 3)
+            dve_c(b1, 0)
+            hT = []
+            for t in range(ahead(s - 1), ahead(s)):
+                hT = hT + pe_hT(t)
             cmm = []
             for ib, half in cm:
                 cmm = cmm + pe_cornermm(ib, half)
             mm = pe_mm(b1, 1)
             weave(mm[0:4] + cmm, pe_mm1(a) + hT)
-            act_hg(a + 3)
+            for t in range(ahead(s - 1), ahead(s)):
+                act_hg(t)
             for ib, half in cm:
                 act_ysb(ib, half)
+            dve_A(b3)
             dve_rs(a2)
             dve_w(a2)
             sp_write(a2)
@@ -453,8 +463,6 @@ def tile_dynamicconvdecoderlayer_pa_kernel(tc, h, x, ww, bw, w2, b2, gamma, beta
             dve_qh(a + 1)
             dve_c(b1, 1)
             act_lt(b0, 3)
-            dve_B(b3)
-            sp_store(b3)
             if 2 <= s < 6:
                 w2_prep(2 * (s - 2))
                 w2_prep(2 * (s - 2) + 1)

@@ -194,7 +194,11 @@ def tile_dynamicconvdecoderlayer_pa_kernel(tc, h, x, ww, bw, w2, b2, gamma, beta
             if not ok(t) or t % 2 == 0:
                 return
             base = t // 2 * 2 * 131072
-            nc.sync.dma_start(out=flat[base:base + 262144].rearrange("(p w) -> p w", w=2048), in_=stages[t // 2 % 2][:].rearrange("p k b n -> p (k b n)"))
+            nc.sync.dma_start(out=flat[base:base + 262144].rearrange("(p w) -> p w", w=2048)[:, 0:1056], in_=stages[t // 2 % 2][:, 0:33, :, :].rearrange("p k b n -> p (k b n)"))
+
+        def sp_zero(t):
+            base = t * 131072
+            nc.sync.dma_start(out=flat[base:base + 262144].rearrange("(p w) -> p w", w=2048)[:, 1056:2048], in_=stages[1][:, 33:SL, :, :].rearrange("p k b n -> p (k b n)"))
 
         def sp_reads(t):
             if not ok(t) or t % 2 == 1:
@@ -207,8 +211,9 @@ def tile_dynamicconvdecoderlayer_pa_kernel(tc, h, x, ww, bw, w2, b2, gamma, beta
 
         def sp_corner(ib, b):
             base = (NB * ib + b) // 2 * 2 * 131072
-            src = flat[base:base + 32 * 2016].rearrange("(i w) -> i w", w=2016)[:, 0:1024].rearrange("i (s c) -> s i c", c=2 * H)
-            nc.sync.dma_start(out=corner[32 * b:32 * b + 32, 32 * b:32 * b + 32, :], in_=src[:, :, H * (b % 2):H * (b % 2) + H])
+            src = flat[base:base + 32 * 2016].rearrange("(i w) -> i w", w=2016)[:, 0:1024].rearrange("i (s c) -> s i c", c=2 * H)[:, :, H * (b % 2):H * (b % 2) + H]
+            for r in (0, 16):
+                nc.sync.dma_start(out=corner[32 * b + r:32 * b + r + 16, 32 * b:32 * b + r + 16, :], in_=src[r:r + 16, 0:r + 16, :])
 
         def act_lc(ib, half):
             lc = p2.tile([P, 8, P], F32, name="lc", tag="lc")
@@ -401,6 +406,9 @@ def tile_dynamicconvdecoderlayer_pa_kernel(tc, h, x, ww, bw, w2, b2, gamma, beta
             if 0 <= s < 3:
                 for t in range(4 * s + 4, 4 * s + 8):
                     ld(t)
+            for t in range(0, NT, 2):
+                if s == max(0, t - 0):
+                    sp_zero(t)
             if s in (0, 1, 3, 4):
                 rt = 2 * s if s < 2 else 2 * s - 2
                 w2_load(rt)
@@ -423,8 +431,9 @@ def tile_dynamicconvdecoderlayer_pa_kernel(tc, h, x, ww, bw, w2, b2, gamma, beta
             act_hf(b0)
             cT = pe_cT(b2t)
             mm = pe_mm(b1, 0)
-            weave(mm[0:3], [])
-            weave(mm[3:8], cT)
+            weave(mm[0:2], [])
+            weave(mm[2:6], cT)
+            weave(mm[6:8], [])
             act_lt(b0, 0)
             act_lt(b0, 1)
             dve_nm(b3)
@@ -454,15 +463,15 @@ def tile_dynamicconvdecoderlayer_pa_kernel(tc, h, x, ww, bw, w2, b2, gamma, beta
             dve_w(a2)
             sp_write(a2)
             act_lt(b0, 2)
+            act_lt(b0, 3)
             dve_xb(b2t)
             weave(mm[4:8], pe_mm2(b2t))
+            dve_qh(a + 1)
+            dve_c(b1, 1)
             for ib, half in ct:
                 if half == 0:
                     act_hcf(ib)
                 act_lc(ib, half)
-            dve_qh(a + 1)
-            dve_c(b1, 1)
-            act_lt(b0, 3)
             if 2 <= s < 6:
                 w2_prep(2 * (s - 2))
                 w2_prep(2 * (s - 2) + 1)

from contextlib import ExitStack
from functools import partial

import concourse.mybir as mybir
from concourse.masks import make_identity

FLOPS = 6576668672
F32 = mybir.dt.float32
BF16 = mybir.dt.bfloat16
U32 = mybir.dt.uint32
U8 = mybir.dt.uint8
FP8X4 = mybir.dt.float8_e4m3fn_x4
ALU = mybir.AluOpType
ACT = mybir.ActivationFunctionType
AX = mybir.AxisListType

P = 128
NB = 4
NI = 4
NT = NB * NI
C = 1024
H = 16
K = 32
R = 64
SL = 64
EPS = 1e-5
LAG = 7


def tile_dynamicconvdecoderlayer_pa_kernel(tc, h, x, ww, bw, w2, b2, gamma, beta, out):
    nc = tc.nc
    with ExitStack() as ctx:
        const = ctx.enter_context(tc.tile_pool(name="const", bufs=1))
        wst = ctx.enter_context(tc.tile_pool(name="wst", bufs=4))
        p2 = ctx.enter_context(tc.tile_pool(name="p2", bufs=2))
        p3 = ctx.enter_context(tc.tile_pool(name="p3", bufs=3))
        hgp = ctx.enter_context(tc.tile_pool(name="hgp", bufs=7))
        p1 = ctx.enter_context(tc.tile_pool(name="p1", bufs=1))
        ps_t = ctx.enter_context(tc.psum_pool(name="ps_t", bufs=3))
        ps_z = ctx.enter_context(tc.psum_pool(name="ps_z", bufs=1))
        ps_c = ctx.enter_context(tc.psum_pool(name="ps_c", bufs=2))
        ps_y = ctx.enter_context(tc.psum_pool(name="ps_y", bufs=2))
        ctx.enter_context(tc.manual_schedule())

        flat = out.rearrange("t b e -> (t b e)")
        T = {}

        def ok(t):
            return 0 <= t < NT

        hbs = [const.tile([P, C], BF16, name="hb%d" % i) for i in range(NT)]
        bw_bc = const.tile([P, H * K], BF16, name="bw_bc")
        b2_bc = const.tile([P, C], BF16, name="b2_bc")
        g_bc = const.tile([P, C], BF16, name="g_bc")
        be_bc = const.tile([P, C], BF16, name="be_bc")

        def ld(t):
            nc.sync.dma_start(out=hbs[t][:], in_=h[P * (t // NB):P * (t // NB) + P, t % NB, :])

        def ld_x(t):
            if not ok(t):
                return
            xt = p3.tile([P, C], BF16, name="xt", tag="xt")
            nc.sync.dma_start(out=xt[:], in_=x[P * (t // NB):P * (t // NB) + P, t % NB, :])
            T[("xt", t)] = xt

        def ld_hc(ib):
            hcb = p1.tile([P, C], BF16, name="hcb", tag="hcb")
            for b in range(NB):
                nc.sync.dma_start(out=hcb[32 * b:32 * b + 32, :], in_=h[P * ib - 32:P * ib, b, :])
            T[("hcb", ib)] = hcb

        raws = []
        for rt in range(4):
            raw = wst.tile([P, C], BF16, name="raw", tag="raw")
            nc.sync.dma_start(out=raw[:], in_=ww[P * rt:P * rt + P, :])
            raws.append(raw)
        ld(0)
        nc.sync.dma_start(out=bw_bc[:], in_=bw.partition_broadcast(P))
        for t in range(1, 4):
            ld(t)

        idf = const.tile([P, 2 * P], F32, name="idf")
        make_identity(nc, idf[:, 0:P])
        nc.vector.tensor_copy(out=idf[:, P:2 * P], in_=idf[:, 0:P])
        msk = const.tile([P, 4], F32, name="msk")
        nc.vector.tensor_reduce(out=msk[:], in_=idf[:, 0:P].rearrange("p (j c) -> p j c", c=32), axis=AX.X, op=ALU.add)
        nhalf = const.tile([P, 1], F32, name="nhalf")
        nc.gpsimd.memset(nhalf[:], -0.5)
        wwq = const.tile([P, 2, 512], U32, name="wwq", align_bytes=64)
        wws = const.tile([P, 2, 512], U8, name="wws", align_bytes=64)
        w2q = const.tile([P, 2, 1024], U32, name="w2q", align_bytes=64)
        w2s = const.tile([P, 2, 1024], U8, name="w2s", align_bytes=64)
        stages = [const.tile([P, SL, 2, H], F32, name="stage%d" % i) for i in range(2)]
        bands = [const.tile([P, P, 2 * H], F32, name="band%d" % i) for i in range(2)]
        corner = const.tile([P, P, H], F32, name="corner")
        for st in stages:
            nc.vector.memset(st[:], 0.0)
        for bt in bands:
            nc.gpsimd.memset(bt[:], 0.0)
        nc.gpsimd.memset(corner[:], 0.0)

        gww = p2.tile([P, 4096], BF16, name="gww", tag="lt", align_bytes=64)
        gww32 = gww[:].bitcast(F32).rearrange("p (g c u) -> p g c u", g=2, u=2)
        for rt in range(4):
            tp = ps_t.tile([P, 4, P], F32, name="tp", tag="tp")
            for gu in range(4):
                g, u = divmod(gu, 2)
                nc.tensor.transpose(tp[:, gu, :], raws[rt][:].bitcast(F32)[:, 256 * g + u:256 * g + 256:2], idf[:, 0:P])
            if rt % 2 == 0:
                nc.vector.tensor_copy(out=gww32[:, :, P * rt:P * rt + P, :], in_=tp[:].rearrange("p (g u) r -> p g r u", g=2))
            else:
                nc.scalar.copy(out=gww32[:, :, P * rt:P * rt + P, :], in_=tp[:].rearrange("p (g u) r -> p g r u", g=2))
        for g in range(2):
            nc.vector.quantize_mx(out=wwq[:, g, :].bitcast(FP8X4), scales=wws[:, g, :], in_=gww[:, 2048 * g:2048 * g + 2048])

        def pe_hT(t):
            if not ok(t):
                return []
            tp = ps_t.tile([P, 4, P], F32, name="tp", tag="tp")
            T[("hT", t)] = tp
            return [partial(nc.tensor.transpose, tp[:, 2 * g + u, :], hbs[t][:].bitcast(F32)[:, 256 * g + u:256 * g + 256:2], idf[:, 0:P]) for g in range(2) for u in range(2)]

        def act_hg(t):
            if not ok(t):
                return
            hg = hgp.tile([P, C], BF16, name="hg", tag="hg", align_bytes=64)
            nc.scalar.copy(out=hg[:].bitcast(F32).rearrange("p (g r u) -> p g r u", g=2, u=2),
                           in_=T[("hT", t)][:].rearrange("p (g u) r -> p g r u", g=2))
            T[("hg", t)] = hg

        def act_hf(t):
            if not ok(t):
                return
            hf = p2.tile([P, C], F32, name="hf", tag="hf")
            nc.scalar.copy(out=hf[:], in_=hbs[t][:])
            T[("hf", t)] = hf

        def dve_qh(t):
            if not ok(t):
                return
            hq = p3.tile([P, 256], U32, name="hq", tag="hq", align_bytes=64)
            hs = p3.tile([P, 256], U8, name="hs", tag="hs", align_bytes=64)
            nc.vector.quantize_mx(out=hq[:].bitcast(FP8X4), scales=hs[:], in_=T[("hg", t)][:])
            T[("hq", t)] = (hq, hs)

        def pe_mm1(t):
            if not ok(t):
                return []
            hq, hs = T[("hq", t)]
            z = ps_z.tile([P, 512], F32, name="z", tag="z")
            T[("z", t)] = z
            return [partial(nc.tensor.matmul_mx, out=z[:], lhsT=hq[:, P * g:P * g + P].bitcast(FP8X4), lhsT_scale=hs[:, P * g:P * g + P],
                            rhs=wwq[:, g, :].bitcast(FP8X4), rhs_scale=wws[:, g, :], start=(g == 0), stop=(g == 1)) for g in range(2)]

        def dve_zb(t):
            if not ok(t):
                return
            zb = p2.tile([P, H, K], F32, name="zb", tag="zb")
            nc.vector.scalar_tensor_tensor(out=zb[:].rearrange("p n k -> p (n k)"), in0=T[("z", t)][:], scalar=-1.0, in1=bw_bc[:], op0=ALU.mult, op1=ALU.subtract)
            T[("zb", t)] = zb

        def dve_max(t):
            if not ok(t):
                return
            mx = p2.tile([P, H], F32, name="mx", tag="mx")
            nc.vector.tensor_reduce(out=mx[:], in_=T[("zb", t)][:], axis=AX.X, op=ALU.min)
            T[("mx", t)] = mx

        def act_exp(t):
            if not ok(t):
                return
            ex = p2.tile([P, H, K], F32, name="ex", tag="ex")
            sums = p2.tile([P, H], F32, name="sums", tag="sums")
            for n in range(H):
                nc.scalar.activation(out=ex[:, n, :], in_=T[("zb", t)][:, n, :], func=ACT.Exp, bias=T[("mx", t)][:, n:n + 1], scale=-1.0, accum_out=sums[:, n:n + 1])
            T[("ex", t)] = ex
            T[("sums", t)] = sums

        def dve_rs(t):
            if not ok(t):
                return
            rs = p2.tile([P, H], F32, name="rs", tag="rs")
            nc.vector.reciprocal(out=rs[:], in_=T[("sums", t)][:])
            T[("rs", t)] = rs

        def dve_w(t):
            if not ok(t):
                return
            nc.vector.tensor_tensor(out=stages[t // 2 % 2][:, 1:1 + K, t % 2, :], in0=T[("ex", t)][:].rearrange("p n k -> p k n"),
                                    in1=T[("rs", t)][:].unsqueeze(1).to_broadcast([P, K, H]), op=ALU.mult)

        def sp_write(t):
            if not ok(t) or t % 2 == 0:
                return
            base = t // 2 * 2 * 131072
            nc.sync.dma_start(out=flat[base:base + 262144].rearrange("(p w) -> p w", w=2048)[:, 0:1056], in_=stages[t // 2 % 2][:, 0:33, :, :].rearrange("p k b n -> p (k b n)"))

        def sp_zero(t):
            base = t * 131072
            nc.sync.dma_start(out=flat[base:base + 262144].rearrange("(p w) -> p w", w=2048)[:, 1056:2048], in_=stages[1][:, 33:SL, :, :].rearrange("p k b n -> p (k b n)"))

        def sp_reads(t):
            if not ok(t) or t % 2 == 1:
                return
            for a in range(8):
                ni = min(47, P - 16 * a)
                base = t * 131072 + 16 * a * 2048 + 512
                src = flat[base:base + ni * 2016].rearrange("(i w) -> i w", w=2016)[:, 512:1024].rearrange("i (s c) -> s i c", c=2 * H)
                nc.sync.dma_start(out=bands[t // 2 % 2][16 * a:16 * a + 16, 16 * a:16 * a + ni, :], in_=src)

        def sp_corner(ib, b):
            base = (NB * ib + b) // 2 * 2 * 131072
            src = flat[base:base + 32 * 2016].rearrange("(i w) -> i w", w=2016)[:, 0:1024].rearrange("i (s c) -> s i c", c=2 * H)[:, :, H * (b % 2):H * (b % 2) + H]
            for r in (0, 16):
                nc.sync.dma_start(out=corner[32 * b + r:32 * b + r + 16, 32 * b:32 * b + r + 16, :], in_=src[r:r + 16, 0:r + 16, :])

        def act_lc(ib, half):
            lc = p2.tile([P, 8, P], F32, name="lc", tag="lc")
            for j in range(2):
                nc.scalar.copy(out=lc[:, 4 * j:4 * j + 4, :].rearrange("p n i -> p i n"), in_=corner[:, :, 8 * half + 4 * j:8 * half + 4 * j + 4])
            T[("lc", ib, half)] = lc

        def act_hcf(ib):
            hcf = p2.tile([P, C], F32, name="hcf", tag="hcf")
            nc.scalar.copy(out=hcf[:], in_=T[("hcb", ib)][:])
            T[("hcf", ib)] = hcf

        def pe_cornermm(ib, half):
            yk = ps_t.tile([P, 512], F32, name="yk", tag="tp")
            T[("yk", ib, half)] = yk
            return [partial(nc.tensor.matmul, out=yk[:, R * m:R * m + R], lhsT=T[("lc", ib, half)][:, m, :], rhs=T[("hcf", ib)][:, R * (8 * half + m):R * (8 * half + m) + R],
                            start=True, stop=True) for m in range(8)]

        def act_ysb(ib, half):
            if half == 0:
                T[("ysb", ib)] = p2.tile([P, C], F32, name="ysb", tag="ysb")
            nc.scalar.copy(out=T[("ysb", ib)][:, 512 * half:512 * half + 512], in_=T[("yk", ib, half)][:])

        def act_lt(t, j):
            if not ok(t):
                return
            if j == 0:
                T[("lt", t)] = p2.tile([P, H, P], F32, name="lt", tag="lt", align_bytes=64)
            lt = T[("lt", t)][:, 4 * j:4 * j + 4, :].rearrange("p n i -> p i n")
            src = bands[t // 2 % 2][:, :, H * (t % 2) + 4 * j:H * (t % 2) + 4 * j + 4]
            turn = 32 * (t % NB)
            copy = nc.scalar.copy if j < 2 else nc.vector.tensor_copy
            copy(out=lt[:, turn:P, :], in_=src[:, 0:P - turn, :])
            if turn > 0:
                copy(out=lt[:, 0:turn, :], in_=src[:, P - turn:P, :])

        def pe_mm(t, half):
            if not ok(t):
                return []
            cd = ps_c.tile([P, 512], F32, name="cd", tag="cd")
            T[("cd", t, half)] = cd
            return [partial(nc.tensor.matmul, out=cd[:, R * m:R * m + R], lhsT=T[("lt", t)][:, 8 * half + m, :], rhs=T[("hf", t)][:, R * (8 * half + m):R * (8 * half + m) + R],
                            start=True, stop=True) for m in range(8)]

        def dve_c(t, half):
            if not ok(t):
                return
            if half == 0:
                T[("cb", t)] = p2.tile([P, C], BF16, name="cb", tag="cb")
            cb = T[("cb", t)][:, 512 * half:512 * half + 512].rearrange("p (u k e) -> p u k e", u=2, e=2)
            cd = T[("cd", t, half)][:].rearrange("p (k u e) -> p u k e", u=2, e=2)
            if t < NB:
                nc.scalar.copy(out=cb, in_=cd)
            else:
                ysb = T[("ysb", t // NB)][:, 512 * half:512 * half + 512].rearrange("p (k u e) -> p u k e", u=2, e=2)
                for u in range(2):
                    nc.vector.scalar_tensor_tensor(out=cb[:, u, :, :], in0=ysb[:, u, :, :], scalar=msk[:, t % NB:t % NB + 1], in1=cd[:, u, :, :], op0=ALU.mult, op1=ALU.add)

        def pe_cT(t):
            if not ok(t):
                return []
            tp = ps_t.tile([P, 4, P], F32, name="tp", tag="tp")
            T[("cT", t)] = tp
            turn = 32 * (t % NB)
            return [partial(nc.tensor.transpose, tp[:, gu, :], T[("cb", t)][:].bitcast(F32)[:, P * gu:P * gu + P], idf[:, turn:turn + P]) for gu in range(4)]

        def act_cg(t):
            if not ok(t):
                return
            cg = p2.tile([P, C], BF16, name="cg", tag="cg", align_bytes=64)
            nc.scalar.copy(out=cg[:].bitcast(F32).rearrange("p (g r u) -> p g r u", g=2, u=2),
                           in_=T[("cT", t)][:].rearrange("p (g u) r -> p g r u", g=2))
            T[("cg", t)] = cg

        def dve_qc(t):
            if not ok(t):
                return
            cq = p2.tile([P, 256], U32, name="cq", tag="cq", align_bytes=64)
            cs = p2.tile([P, 256], U8, name="cs", tag="cs", align_bytes=64)
            nc.vector.quantize_mx(out=cq[:].bitcast(FP8X4), scales=cs[:], in_=T[("cg", t)][:])
            T[("cq", t)] = (cq, cs)

        def pe_mm2(t):
            if not ok(t):
                return []
            cq, cs = T[("cq", t)]
            passes = []
            for e2 in range(2):
                yp = ps_y.tile([P, 512], F32, name="yp", tag="yp")
                T[("yp", t, e2)] = yp
                for g in range(2):
                    passes.append(partial(nc.tensor.matmul_mx, out=yp[:], lhsT=cq[:, P * g:P * g + P].bitcast(FP8X4), lhsT_scale=cs[:, P * g:P * g + P],
                                          rhs=w2q[:, g, 512 * e2:512 * e2 + 512].bitcast(FP8X4), rhs_scale=w2s[:, g, 512 * e2:512 * e2 + 512],
                                          start=(g == 0), stop=(g == 1)))
            return passes

        def weave(narrow, others):
            n = max(len(narrow), len(others))
            for i in range(n):
                for group in (narrow, others):
                    for k in range(i * len(group) // n, (i + 1) * len(group) // n):
                        group[k]()

        def dve_xb(t):
            if not ok(t):
                return
            xb = p2.tile([P, C], F32, name="xb", tag="xb")
            nc.vector.tensor_tensor(out=xb[:], in0=T[("xt", t)][:], in1=b2_bc[:], op=ALU.add)
            T[("xb", t)] = xb

        def dve_v(t):
            if not ok(t):
                return
            v = p2.tile([P, C], F32, name="v", tag="v")
            s2 = p2.tile([P, 2], F32, name="s2", tag="s2")
            xb = T[("xb", t)]
            for e2 in range(2):
                nc.vector.scalar_tensor_tensor(out=v[:, 512 * e2:512 * e2 + 512], in0=T[("yp", t, e2)][:], scalar=1.0,
                                               in1=xb[:, 512 * e2:512 * e2 + 512], op0=ALU.mult, op1=ALU.add, accum_out=s2[:, e2:e2 + 1])
            T[("v", t)] = v
            T[("s2", t)] = s2

        def dve_nm(t):
            if not ok(t):
                return
            s2 = T[("s2", t)]
            nm = p2.tile([P, 1], F32, name="nm", tag="nm")
            nc.vector.tensor_scalar(out=nm[:], in0=s2[:, 0:1], scalar1=s2[:, 1:2], scalar2=-1.0 / C, op0=ALU.add, op1=ALU.mult)
            T[("nm", t)] = nm

        def act_sq(t):
            if not ok(t):
                return
            junk = p1.tile([P, C], BF16, name="junk", tag="junk")
            ss = p2.tile([P, 1], F32, name="ss", tag="ss")
            nc.scalar.activation(out=junk[:], in_=T[("v", t)][:], func=ACT.Square, bias=T[("nm", t)][:], scale=1.0, accum_out=ss[:])
            T[("ss", t)] = ss

        def pool_rstd(t):
            if not ok(t):
                return
            ve = p2.tile([P, 1], F32, name="ve", tag="ve")
            nc.gpsimd.tensor_scalar(out=ve[:], in0=T[("ss", t)][:], scalar1=1.0 / C, scalar2=EPS, op0=ALU.mult, op1=ALU.add)
            rstd = p2.tile([P, 1], F32, name="rstd", tag="rstd")
            nc.gpsimd.tensor_tensor(out=rstd[:], in0=ve[:], in1=nhalf[:], op=ALU.pow)
            T[("rstd", t)] = rstd

        def dve_A(t):
            if not ok(t):
                return
            t1 = p2.tile([P, C], F32, name="t1", tag="t1")
            nc.vector.scalar_tensor_tensor(out=t1[:], in0=T[("v", t)][:], scalar=T[("nm", t)][:], in1=g_bc[:], op0=ALU.add, op1=ALU.mult)
            T[("t1", t)] = t1

        def dve_B(t):
            if not ok(t):
                return
            t1 = T[("t1", t)]
            nc.vector.scalar_tensor_tensor(out=t1[:], in0=t1[:], scalar=T[("rstd", t)][:], in1=be_bc[:], op0=ALU.mult, op1=ALU.add)

        def sp_store(t):
            if not ok(t):
                return
            nc.sync.dma_start(out=out[P * (t // NB):P * (t // NB) + P, t % NB, :], in_=T[("t1", t)][:])

        def w2_load(rt):
            raw = wst.tile([P, C], BF16, name="raw", tag="raw")
            nc.sync.dma_start(out=raw[:], in_=w2[P * rt:P * rt + P, :])
            T[("raw", rt)] = raw

        def w2_prep(rt):
            if rt == 0:
                T["gw2"] = [p2.tile([P, 4096], BF16, name="gw2", tag="lt", align_bytes=64) for g in range(2)]
            tp = ps_t.tile([P, 4, P], F32, name="tp", tag="tp")
            for gu in range(4):
                g, u = divmod(gu, 2)
                nc.tensor.transpose(tp[:, gu, :], T[("raw", rt)][:].bitcast(F32)[:, 256 * g + u:256 * g + 256:2], idf[:, 0:P])
            for g in range(2):
                nc.scalar.copy(out=T["gw2"][g][:].bitcast(F32).rearrange("p (c u) -> p c u", u=2)[:, P * rt:P * rt + P, :],
                               in_=tp[:, 2 * g:2 * g + 2, :].rearrange("p u r -> p r u"))

        def ahead(s):
            return s + 4 + min(max(s, 0), 3)

        for s in range(-3, NT + LAG + 5):
            a, a1, a2 = s, s - 1, s - 2
            b0, b1, b2t, b3, b4 = s - LAG, s - LAG - 1, s - LAG - 2, s - LAG - 3, s - LAG - 4
            ct = [(ib, half) for ib in range(1, NI) for half in range(2) if s == 4 * ib + 6 + half]
            cm = [(ib, half) for ib in range(1, NI) for half in range(2) if s == 4 * ib + 7 + half]
            if 0 <= s < 3:
                for t in range(4 * s + 4, 4 * s + 8):
                    ld(t)
            for t in range(0, NT, 2):
                if s == max(0, t - 0):
                    sp_zero(t)
            if s in (0, 1, 3, 4):
                rt = 2 * s if s < 2 else 2 * s - 2
                w2_load(rt)
                w2_load(rt + 1)
            if s == 2:
                nc.sync.dma_start(out=b2_bc[:], in_=b2.partition_broadcast(P))
            if s == 3:
                nc.sync.dma_start(out=g_bc[:], in_=gamma.partition_broadcast(P))
                nc.sync.dma_start(out=be_bc[:], in_=beta.partition_broadcast(P))
            ld_x(b0)
            for ib in range(1, NI):
                if s == 4 * ib + 4:
                    ld_hc(ib)
            for t in range(0, NT, 2):
                if s == t + (4 if t < 4 else LAG - 2):
                    sp_reads(t)

            dve_zb(a1)
            dve_v(b3)
            act_hf(b0)
            cT = pe_cT(b2t)
            mm = pe_mm(b1, 0)
            weave(mm[0:2], [])
            weave(mm[2:6], cT)
            weave(mm[6:8], [])
            act_lt(b0, 0)
            act_lt(b0, 1)
            dve_nm(b3)
            act_cg(b2t)
            act_sq(b3)
            pool_rstd(b3)
            dve_B(b4)
            sp_store(b4)
            dve_max(a1)
            act_exp(a1)
            dve_qc(b2t)
            dve_c(b1, 0)
            hT = []
            for t in range(ahead(s - 1), ahead(s)):
                hT = hT + pe_hT(t)
            cmm = []
            for ib, half in cm:
                cmm = cmm + pe_cornermm(ib, half)
            mm = pe_mm(b1, 1)
            weave(mm[0:4] + cmm, pe_mm1(a) + hT)
            for t in range(ahead(s - 1), ahead(s)):
                act_hg(t)
            for ib, half in cm:
                act_ysb(ib, half)
            dve_A(b3)
            dve_rs(a2)
            dve_w(a2)
            sp_write(a2)
            act_lt(b0, 2)
            act_lt(b0, 3)
            dve_xb(b2t)
            weave(mm[4:8], pe_mm2(b2t))
            dve_qh(a + 1)
            dve_c(b1, 1)
            for ib, half in ct:
                if half == 0:
                    act_hcf(ib)
                act_lc(ib, half)
            if 2 <= s < 6:
                w2_prep(2 * (s - 2))
                w2_prep(2 * (s - 2) + 1)
            if s == 6:
                for g in range(2):
                    nc.vector.quantize_mx(out=w2q[:, g, :].bitcast(FP8X4), scales=w2s[:, g, :], in_=T["gw2"][g][:])
            for ib in range(1, NI):
                if s == 4 * ib + 5:
                    for b in range(NB):
                        sp_corner(ib, b)
